import numpy as np
import ml_dtypes


def mxq(x, axis, fmt="e4m3"):
    dtype, down = {"e4m3": (ml_dtypes.float8_e4m3fn, 7), "e5m2": (ml_dtypes.float8_e5m2, 14)}[fmt]
    v = np.moveaxis(np.asarray(x, np.float32).astype(ml_dtypes.bfloat16).astype(np.float64), axis, -1)
    blocks = v.reshape(v.shape[:-1] + (-1, 32))
    amax = np.abs(blocks).max(-1, keepdims=True)
    byte = np.maximum(np.where(amax > 0, np.frexp(amax)[1] - 1 + 127, 0) - down, 1)
    scale = np.exp2(byte - 127.0)
    codes = (blocks / scale).astype(np.float32).astype(dtype).astype(np.float64)
    return np.moveaxis((codes * scale).reshape(v.shape), -1, axis)


WIDE = False


def mx_kscale(k):
    if not WIDE:
        return np.ones(k)
    levels = np.array([10, -10, 5, -5, 0])
    a = np.random.permutation(np.resize(levels, k // 512 * 4)).reshape(k // 512, 4)
    idx = np.arange(k)
    return np.exp2(a[idx // 512, idx % 128 // 32])


BF16 = ml_dtypes.bfloat16


def bf(x):
    return np.asarray(x, np.float32).astype(BF16)


def f64(x):
    return np.asarray(x).astype(np.float64)


B, S, D, F, R = 4, 1024, 512, 512, 128
SCALING = 2.0


def silu(v):
    return v / (1.0 + np.exp(-v))


def setup_inputs():
    s = mx_kscale(D)
    return {
        "x": bf(np.random.standard_normal((B, S, D)) * s),
        "w1": bf(np.random.standard_normal((F, D)) / np.sqrt(D) / s),
        "w3": bf(np.random.standard_normal((F, D)) / np.sqrt(D) / s),
        "xa1": bf(np.random.standard_normal((B, S, R))),
        "xa3": bf(np.random.standard_normal((B, S, R))),
        "lora_B1": bf(np.random.standard_normal((F, R)) * 0.25 / np.sqrt(R)),
        "lora_B3": bf(np.random.standard_normal((F, R)) * 0.25 / np.sqrt(R)),
        "lora_A2": bf(np.random.standard_normal((R, F)) / np.sqrt(F)),
    }


def reference(x, w1, w3, xa1, xa3, lora_B1, lora_B3, lora_A2):
    xq = mxq(f64(x), 2, "e4m3")
    h1 = (xq @ mxq(f64(w1), 1, "e4m3").T) + (f64(xa1) @ f64(lora_B1).T) * SCALING
    h3 = (xq @ mxq(f64(w3), 1, "e4m3").T) + (f64(xa3) @ f64(lora_B3).T) * SCALING
    g = silu(h1) * h3
    ga2 = mxq(g, 2, "e4m3") @ mxq(f64(lora_A2), 1, "e4m3").T
    return g, ga2

@@ -1,0 +1,373 @@
+from contextlib import ExitStack
+
+import concourse.mybir as mybir
+from concourse.masks import make_identity
+
+F32 = mybir.dt.float32
+BF16 = mybir.dt.bfloat16
+U32 = mybir.dt.uint32
+U8 = mybir.dt.uint8
+FP8X4 = mybir.dt.float8_e4m3fn_x4
+ACT = mybir.ActivationFunctionType
+ALU = mybir.AluOpType
+
+P = 128
+TOKENS = 4096
+D = 512
+F = 512
+R = 128
+NT = TOKENS // P
+TPG = 4
+NG = NT // TPG
+FLOPS = 2 * TOKENS * (2 * D * F + 2 * R * F + F * R)
+
+
+def tile_feedforward_pa_t_kernel(
+    tc, x, w1, w3, xa1, xa3, lora_B1, lora_B3, lora_A2, out_0, out_1
+):
+    nc = tc.nc
+    xv = x.flatten_outer_dims().rearrange("(p j) d -> p (j d)", j=NT)
+    xa1v = xa1.flatten_outer_dims().rearrange("(p j) r -> p (j r)", j=NT)
+    xa3v = xa3.flatten_outer_dims().rearrange("(p j) r -> p (j r)", j=NT)
+    gv = out_0.flatten_outer_dims().rearrange("(p j) f -> p (j f)", j=NT)
+    ov = out_1.flatten_outer_dims().rearrange("(p j) r -> p (j r)", j=NT)
+
+    with ExitStack() as ctx:
+        ctx.enter_context(tc.manual_schedule())
+        keep = ctx.enter_context(tc.tile_pool(name="keep", bufs=1))
+        rot2 = ctx.enter_context(tc.tile_pool(name="rot2", bufs=2))
+        rot3 = ctx.enter_context(tc.tile_pool(name="rot3", bufs=3))
+        ps1 = ctx.enter_context(tc.psum_pool(name="ps1", bufs=1))
+        ps2 = ctx.enter_context(tc.psum_pool(name="ps2", bufs=2))
+
+        w_sb = {}
+        for k in (1, 3):
+            w_sb[k] = keep.tile([P, 4 * D], BF16, name="w_sb%d" % k)
+        b_sb = keep.tile([P, 2 * 4 * R], BF16, name="b_sb")
+        a_sb = keep.tile([P, F], BF16, name="a_sb")
+        x_sb = {}
+        xa_sb = {}
+        for g in range(NG):
+            x_sb[g] = keep.tile([P, TPG * D], BF16, name="x_sb%d" % g)
+            xa_sb[g] = keep.tile([P, 2 * TPG * R], BF16, name="xa_sb%d" % g)
+
+        def load_w(k, w):
+            nc.sync.dma_start(
+                out=w_sb[k][:].rearrange("p (c d) -> p c d", c=4),
+                in_=w.rearrange("(c p) d -> p c d", p=P),
+            )
+
+        def load_x(g):
+            nc.sync.dma_start(out=x_sb[g][:], in_=xv[:, TPG * D * g : TPG * D * (g + 1)])
+
+        def load_xa(g):
+            n = TPG * R
+            nc.sync.dma_start(out=xa_sb[g][:, 0:n], in_=xa1v[:, n * g : n * (g + 1)])
+            nc.sync.dma_start(out=xa_sb[g][:, n : 2 * n], in_=xa3v[:, n * g : n * (g + 1)])
+
+        load_w(1, w1)
+        load_x(0)
+        load_w(3, w3)
+        load_xa(0)
+        nc.sync.dma_start(
+            out=b_sb[:, 0 : 4 * R].rearrange("p (c r) -> p c r", c=4),
+            in_=lora_B1.rearrange("(c p) r -> p c r", p=P),
+        )
+        nc.sync.dma_start(
+            out=b_sb[:, 4 * R : 8 * R].rearrange("p (c r) -> p c r", c=4),
+            in_=lora_B3.rearrange("(c p) r -> p c r", p=P),
+        )
+        load_x(1)
+        nc.sync.dma_start(out=a_sb[:], in_=lora_A2)
+        load_xa(1)
+        for g in range(2, NG):
+            load_x(g)
+            load_xa(g)
+
+        ident_f = keep.tile([P, P], F32, name="ident_f")
+        make_identity(nc, ident_f[:])
+        ident_b = keep.tile([P, P], BF16, name="ident_b")
+        make_identity(nc, ident_b[:])
+
+        def word_transposes(words, bank):
+            for a in range(2):
+                for u in range(2):
+                    c0 = 256 * a + 128 * u
+                    nc.tensor.transpose(bank[:, a, u, :], words[:, c0 : c0 + 128], ident_f[:])
+
+        def word_copy(copy, words, bank):
+            copy(
+                out=words.rearrange("p (a r u) -> p a r u", a=2, u=2),
+                in_=bank[:].rearrange("p a u r -> p a r u"),
+            )
+
+        wg = {}
+        wc = {}
+        ws = {}
+        wbank = {}
+        for k in (1, 3):
+            wg[k] = keep.tile([P, 4 * F], BF16, name="wg%d" % k, align_bytes=64)
+            wc[k] = keep.tile([P, F], U32, name="wc%d" % k, align_bytes=64)
+            ws[k] = keep.tile([P, F], U8, name="ws%d" % k, align_bytes=64)
+        xg = {}
+        xc = {}
+        xs = {}
+        xaT = {}
+        xbank = {}
+        abank = {}
+        for g in range(NG):
+            xc[g] = keep.tile([P, TPG * P], U32, name="xc%d" % g, align_bytes=64)
+            xs[g] = keep.tile([P, TPG * P], U8, name="xs%d" % g, align_bytes=64)
+            xaT[g] = keep.tile([P, 2 * TPG * P], BF16, name="xaT%d" % g)
+
+        def w_transposes(k, tags):
+            for h in range(2):
+                wbank[(k, h)] = ps1.tile([P, 2, 2, P], F32, name="wbank", tag=tags[h])
+                word_transposes(w_sb[k][:].bitcast(F32)[:, 512 * h : 512 * h + 512], wbank[(k, h)])
+
+        def w_copy(k, h, copy):
+            word_copy(copy, wg[k][:].bitcast(F32)[:, 512 * h : 512 * h + 512], wbank[(k, h)])
+
+        def w_quant(k):
+            nc.vector.quantize_mx(out=wc[k][:].bitcast(FP8X4), scales=ws[k][:], in_=wg[k][:])
+
+        def x_transposes(g, h):
+            if not 0 <= g < NG:
+                return
+            xbank[(g, h)] = ps2.tile([P, 2, 2, P], F32, name="xbank", tag="misc")
+            word_transposes(x_sb[g][:].bitcast(F32)[:, 512 * h : 512 * h + 512], xbank[(g, h)])
+
+        def x_copy(g, h, copy):
+            if not 0 <= g < NG:
+                return
+            if h == 0:
+                xg[g] = rot2.tile([P, 4 * TPG * P], BF16, name="xg", tag="xg", align_bytes=64)
+            word_copy(copy, xg[g][:].bitcast(F32)[:, 512 * h : 512 * h + 512], xbank[(g, h)])
+
+        def x_quant(g):
+            if not 0 <= g < NG:
+                return
+            nc.vector.quantize_mx(out=xc[g][:].bitcast(FP8X4), scales=xs[g][:], in_=xg[g][:])
+
+        def xa_transposes(g):
+            if not 0 <= g < NG:
+                return
+            abank[g] = ps2.tile([P, 2 * TPG * P], BF16, name="abank", tag="misc")
+            for i in range(2 * TPG):
+                nc.tensor.transpose(
+                    abank[g][:, P * i : P * (i + 1)], xa_sb[g][:, R * i : R * (i + 1)], ident_b[:]
+                )
+
+        def xa_copy(g, copy):
+            if not 0 <= g < NG:
+                return
+            copy(out=xaT[g][:], in_=abank[g][:])
+
+        w_transposes(1, ("mx1", "mx3"))
+        x_transposes(0, 0)
+        x_transposes(0, 1)
+        w_transposes(3, ("l1", "l3"))
+        w_copy(1, 0, nc.scalar.copy)
+        w_copy(1, 1, nc.vector.tensor_copy)
+        x_copy(0, 0, nc.scalar.copy)
+        x_copy(0, 1, nc.vector.tensor_copy)
+        w_quant(1)
+        w_copy(3, 0, nc.scalar.copy)
+        w_copy(3, 1, nc.vector.tensor_copy)
+        x_quant(0)
+        xa_transposes(0)
+        xa_copy(0, nc.scalar.copy)
+        bbank = ps1.tile([P, 2 * F], BF16, name="bbank", tag="gt")
+        for i in range(8):
+            nc.tensor.transpose(bbank[:, P * i : P * (i + 1)], b_sb[:, R * i : R * (i + 1)], ident_b[:])
+        bT = keep.tile([P, 2 * F], BF16, name="bT")
+        nc.scalar.copy(out=bT[:], in_=bbank[:])
+        w_quant(3)
+        a2bank = ps1.tile([P, 4, P], BF16, name="a2bank", tag="o")
+        for c in range(4):
+            nc.tensor.transpose(a2bank[:, c, :], a_sb[:, P * c : P * (c + 1)], ident_b[:])
+        ag = keep.tile([P, 4 * R], BF16, name="ag", align_bytes=64)
+        ac = keep.tile([P, R], U32, name="ac", align_bytes=64)
+        asc = keep.tile([P, R], U8, name="asc", align_bytes=64)
+
+        def a2_copy():
+            nc.vector.tensor_copy(
+                out=ag[:].rearrange("p (r c) -> p r c", c=4),
+                in_=a2bank[:].rearrange("p c r -> p r c"),
+            )
+
+        def a2_quant():
+            nc.vector.quantize_mx(out=ac[:].bitcast(FP8X4), scales=asc[:], in_=ag[:])
+
+        mx = {}
+        lo = {}
+        m_sb = {}
+        h_sb = {}
+        s_sb = {}
+        g_sb = {}
+        gbank = {}
+        gg = {}
+        gc = {}
+        gs = {}
+        obank = {}
+
+        def ok(t):
+            return 0 <= t < NT
+
+        def mx_pass(k, t):
+            if not ok(t):
+                return
+            g, j = divmod(t, TPG)
+            mx[(k, t)] = ps1.tile([P, F], F32, name="mx%d" % k, tag="mx%d" % k)
+            nc.tensor.matmul_mx(
+                out=mx[(k, t)][:],
+                lhsT=xc[g][:, P * j : P * (j + 1)].bitcast(FP8X4),
+                lhsT_scale=xs[g][:, P * j : P * (j + 1)],
+                rhs=wc[k][:].bitcast(FP8X4),
+                rhs_scale=ws[k][:],
+                start=True,
+                stop=True,
+            )
+
+        def lora(k, t):
+            if not ok(t):
+                return
+            g, j = divmod(t, TPG)
+            half = 0 if k == 1 else 1
+            i = TPG * half + j
+            lo[(k, t)] = ps1.tile([P, F], F32, name="l%d" % k, tag="l%d" % k)
+            nc.tensor.matmul(
+                out=lo[(k, t)][:],
+                lhsT=xaT[g][:, P * i : P * (i + 1)],
+                rhs=bT[:, F * half : F * (half + 1)],
+                start=True,
+                stop=True,
+            )
+
+        def mx_out(k, t):
+            if not ok(t):
+                return
+            m_sb[(k, t)] = rot3.tile([P, F], F32, name="m%d" % k, tag="m%d" % k)
+            nc.scalar.copy(out=m_sb[(k, t)][:], in_=mx[(k, t)][:])
+
+        def add(k, t):
+            if not ok(t):
+                return
+            h_sb[(k, t)] = rot3.tile([P, F], F32, name="h%d" % k, tag="h%d" % k)
+            nc.vector.scalar_tensor_tensor(
+                out=h_sb[(k, t)][:],
+                in0=lo[(k, t)][:],
+                scalar=2.0,
+                in1=m_sb[(k, t)][:],
+                op0=ALU.mult,
+                op1=ALU.add,
+            )
+
+        def silu(t):
+            if not ok(t):
+                return
+            s_sb[t] = rot3.tile([P, F], F32, name="s1", tag="s1")
+            nc.scalar.activation(out=s_sb[t][:], in_=h_sb[(1, t)][:], func=ACT.Silu)
+
+        def gate(t):
+            if not ok(t):
+                return
+            g, j = divmod(t, TPG)
+            if j == 0:
+                g_sb[g] = rot3.tile([P, TPG * F], F32, name="g_sb", tag="g_sb")
+            nc.gpsimd.tensor_tensor(
+                out=g_sb[g][:, F * j : F * (j + 1)], in0=s_sb[t][:], in1=h_sb[(3, t)][:], op=ALU.mult
+            )
+            if j % 2 == 1:
+                nc.sync.dma_start(
+                    out=gv[:, F * (t - 1) : F * (t + 1)], in_=g_sb[g][:, F * (j - 1) : F * (j + 1)]
+                )
+
+        def g_transposes(t):
+            if not ok(t):
+                return
+            g, j = divmod(t, TPG)
+            gbank[t] = ps1.tile([P, 4, P], F32, name="gbank", tag="gt")
+            for c in range(4):
+                c0 = F * j + P * c
+                nc.tensor.transpose(gbank[t][:, c, :], g_sb[g][:, c0 : c0 + P], ident_f[:])
+
+        def g_copy(t):
+            if not ok(t):
+                return
+            gg[t] = rot3.tile([P, 4 * P], BF16, name="gg", tag="gg", align_bytes=64)
+            nc.vector.tensor_copy(
+                out=gg[t][:].rearrange("p (r c) -> p r c", c=4),
+                in_=gbank[t][:].rearrange("p c r -> p r c"),
+            )
+
+        def g_quant(t):
+            if not ok(t):
+                return
+            gc[t] = rot3.tile([P, P], U32, name="gc", tag="gc", align_bytes=64)
+            gs[t] = rot3.tile([P, P], U8, name="gs", tag="gs", align_bytes=64)
+            nc.vector.quantize_mx(out=gc[t][:].bitcast(FP8X4), scales=gs[t][:], in_=gg[t][:])
+
+        def ga2(t):
+            if not ok(t):
+                return
+            g, j = divmod(t, TPG)
+            if j == 0:
+                obank[g] = ps1.tile([P, TPG, R], F32, name="obank", tag="o")
+            nc.tensor.matmul_mx(
+                out=obank[g][:, j, :],
+                lhsT=gc[t][:].bitcast(FP8X4),
+                lhsT_scale=gs[t][:],
+                rhs=ac[:].bitcast(FP8X4),
+                rhs_scale=asc[:],
+                start=True,
+                stop=True,
+            )
+
+        def o_out(g):
+            if not 0 <= g < NG:
+                return
+            o_sb = rot2.tile([P, TPG * R], F32, name="o_sb", tag="o_sb")
+            nc.scalar.copy(out=o_sb[:], in_=obank[g][:].rearrange("p j r -> p (j r)"))
+            nc.sync.dma_start(out=ov[:, TPG * R * g : TPG * R * (g + 1)], in_=o_sb[:])
+
+        for t in range(-2, NT + 3):
+            g, r = divmod(t, TPG)
+            mx_out(1, t + 1)
+            add(1, t)
+            g_transposes(t - 2)
+            if r == 3 and t > 0:
+                x_transposes(g + 2, 0)
+            if r == 0:
+                if t == 0:
+                    x_transposes(1, 0)
+                x_transposes(g + 1, 1)
+            if r == 1 and t > 0:
+                xa_transposes(g + 1)
+            lora(1, t + 1)
+            mx_pass(1, t + 2)
+            mx_out(3, t + 1)
+            mx_pass(3, t + 2)
+            add(3, t)
+            g_quant(t - 3)
+            ga2(t - 3)
+            lora(3, t + 1)
+            if t == -1:
+                a2_copy()
+            if t == 0:
+                a2_quant()
+            if r == 1 and t > 0:
+                x_quant(g + 1)
+            if r == 2 and t > 0:
+                xa_copy(g + 1, nc.vector.tensor_copy)
+            silu(t)
+            if r == 3 and t > 0:
+                x_copy(g + 2, 0, nc.scalar.copy)
+            if r == 0:
+                if t == 0:
+                    x_copy(1, 0, nc.scalar.copy)
+                x_copy(g + 1, 1, nc.scalar.copy)
+            if r == 2:
+                o_out(g - 1)
+            gate(t)
+            g_copy(t - 2)

@@ -33,7 +33,6 @@ def tile_feedforward_pa_t_kernel(
     ov = out_1.flatten_outer_dims().rearrange("(p j) r -> p (j r)", j=NT)
 
     with ExitStack() as ctx:
-        ctx.enter_context(tc.manual_schedule())
         keep = ctx.enter_context(tc.tile_pool(name="keep", bufs=1))
         rot2 = ctx.enter_context(tc.tile_pool(name="rot2", bufs=2))
         rot3 = ctx.enter_context(tc.tile_pool(name="rot3", bufs=3))

@@ -17,8 +17,9 @@ D = 512
 F = 512
 R = 128
 NT = TOKENS // P
-TPG = 4
-NG = NT // TPG
+NP = NT // 2
+NG = NT // 4
+WARM = 5
 FLOPS = 2 * TOKENS * (2 * D * F + 2 * R * F + F * R)
 
 
@@ -33,9 +34,10 @@ def tile_feedforward_pa_t_kernel(
     ov = out_1.flatten_outer_dims().rearrange("(p j) r -> p (j r)", j=NT)
 
     with ExitStack() as ctx:
+        ctx.enter_context(tc.manual_schedule())
         keep = ctx.enter_context(tc.tile_pool(name="keep", bufs=1))
-        rot2 = ctx.enter_context(tc.tile_pool(name="rot2", bufs=2))
         rot3 = ctx.enter_context(tc.tile_pool(name="rot3", bufs=3))
+        rot6 = ctx.enter_context(tc.tile_pool(name="rot6", bufs=6))
         ps1 = ctx.enter_context(tc.psum_pool(name="ps1", bufs=1))
         ps2 = ctx.enter_context(tc.psum_pool(name="ps2", bufs=2))
 
@@ -47,40 +49,44 @@ def tile_feedforward_pa_t_kernel(
         x_sb = {}
         xa_sb = {}
         for g in range(NG):
-            x_sb[g] = keep.tile([P, TPG * D], BF16, name="x_sb%d" % g)
-            xa_sb[g] = keep.tile([P, 2 * TPG * R], BF16, name="xa_sb%d" % g)
+            x_sb[g] = keep.tile([P, 4 * D], BF16, name="x_sb%d" % g)
+            xa_sb[g] = keep.tile([P, 2 * 4 * R], BF16, name="xa_sb%d" % g)
 
-        def load_w(k, w):
+        def load_w(k, w, h):
             nc.sync.dma_start(
-                out=w_sb[k][:].rearrange("p (c d) -> p c d", c=4),
-                in_=w.rearrange("(c p) d -> p c d", p=P),
+                out=w_sb[k][:, 2 * D * h : 2 * D * (h + 1)].rearrange("p (c d) -> p c d", c=2),
+                in_=w[2 * P * h : 2 * P * (h + 1), :].rearrange("(c p) d -> p c d", p=P),
             )
 
-        def load_x(g):
-            nc.sync.dma_start(out=x_sb[g][:], in_=xv[:, TPG * D * g : TPG * D * (g + 1)])
+        def load_x(c0, c1):
+            g = c0 // (4 * D)
+            nc.sync.dma_start(out=x_sb[g][:, c0 - 4 * D * g : c1 - 4 * D * g], in_=xv[:, c0:c1])
 
         def load_xa(g):
-            n = TPG * R
+            n = 4 * R
             nc.sync.dma_start(out=xa_sb[g][:, 0:n], in_=xa1v[:, n * g : n * (g + 1)])
             nc.sync.dma_start(out=xa_sb[g][:, n : 2 * n], in_=xa3v[:, n * g : n * (g + 1)])
 
-        load_w(1, w1)
-        load_x(0)
-        load_w(3, w3)
+        def load_b(half, b):
+            nc.sync.dma_start(
+                out=b_sb[:, 4 * R * half : 4 * R * (half + 1)].rearrange("p (c r) -> p c r", c=4),
+                in_=b.rearrange("(c p) r -> p c r", p=P),
+            )
+
+        load_w(1, w1, 0)
+        load_w(1, w1, 1)
+        load_x(0, 2 * D)
         load_xa(0)
-        nc.sync.dma_start(
-            out=b_sb[:, 0 : 4 * R].rearrange("p (c r) -> p c r", c=4),
-            in_=lora_B1.rearrange("(c p) r -> p c r", p=P),
-        )
-        nc.sync.dma_start(
-            out=b_sb[:, 4 * R : 8 * R].rearrange("p (c r) -> p c r", c=4),
-            in_=lora_B3.rearrange("(c p) r -> p c r", p=P),
-        )
-        load_x(1)
-        nc.sync.dma_start(out=a_sb[:], in_=lora_A2)
+        load_w(3, w3, 0)
+        load_w(3, w3, 1)
+        load_b(0, lora_B1)
+        load_b(1, lora_B3)
+        load_x(2 * D, 4 * D)
+        load_x(4 * D, 8 * D)
         load_xa(1)
+        nc.sync.dma_start(out=a_sb[:], in_=lora_A2)
         for g in range(2, NG):
-            load_x(g)
+            load_x(4 * D * g, 4 * D * (g + 1))
             load_xa(g)
 
         ident_f = keep.tile([P, P], F32, name="ident_f")
@@ -100,6 +106,12 @@ def tile_feedforward_pa_t_kernel(
                 in_=bank[:].rearrange("p a u r -> p a r u"),
             )
 
+        def okp(q):
+            return 0 <= q < NP
+
+        def ok(t):
+            return 0 <= t < NT
+
         wg = {}
         wc = {}
         ws = {}
@@ -108,21 +120,10 @@ def tile_feedforward_pa_t_kernel(
             wg[k] = keep.tile([P, 4 * F], BF16, name="wg%d" % k, align_bytes=64)
             wc[k] = keep.tile([P, F], U32, name="wc%d" % k, align_bytes=64)
             ws[k] = keep.tile([P, F], U8, name="ws%d" % k, align_bytes=64)
-        xg = {}
-        xc = {}
-        xs = {}
-        xaT = {}
-        xbank = {}
-        abank = {}
-        for g in range(NG):
-            xc[g] = keep.tile([P, TPG * P], U32, name="xc%d" % g, align_bytes=64)
-            xs[g] = keep.tile([P, TPG * P], U8, name="xs%d" % g, align_bytes=64)
-            xaT[g] = keep.tile([P, 2 * TPG * P], BF16, name="xaT%d" % g)
 
-        def w_transposes(k, tags):
-            for h in range(2):
-                wbank[(k, h)] = ps1.tile([P, 2, 2, P], F32, name="wbank", tag=tags[h])
-                word_transposes(w_sb[k][:].bitcast(F32)[:, 512 * h : 512 * h + 512], wbank[(k, h)])
+        def w_transposes(k, h):
+            wbank[(k, h)] = ps2.tile([P, 2, 2, P], F32, name="wbank", tag="gt")
+            word_transposes(w_sb[k][:].bitcast(F32)[:, 512 * h : 512 * h + 512], wbank[(k, h)])
 
         def w_copy(k, h, copy):
             word_copy(copy, wg[k][:].bitcast(F32)[:, 512 * h : 512 * h + 512], wbank[(k, h)])
@@ -130,73 +131,89 @@ def tile_feedforward_pa_t_kernel(
         def w_quant(k):
             nc.vector.quantize_mx(out=wc[k][:].bitcast(FP8X4), scales=ws[k][:], in_=wg[k][:])
 
-        def x_transposes(g, h):
-            if not 0 <= g < NG:
-                return
-            xbank[(g, h)] = ps2.tile([P, 2, 2, P], F32, name="xbank", tag="misc")
-            word_transposes(x_sb[g][:].bitcast(F32)[:, 512 * h : 512 * h + 512], xbank[(g, h)])
+        bT = {}
+        bbank = {}
 
-        def x_copy(g, h, copy):
-            if not 0 <= g < NG:
-                return
-            if h == 0:
-                xg[g] = rot2.tile([P, 4 * TPG * P], BF16, name="xg", tag="xg", align_bytes=64)
-            word_copy(copy, xg[g][:].bitcast(F32)[:, 512 * h : 512 * h + 512], xbank[(g, h)])
-
-        def x_quant(g):
-            if not 0 <= g < NG:
-                return
-            nc.vector.quantize_mx(out=xc[g][:].bitcast(FP8X4), scales=xs[g][:], in_=xg[g][:])
-
-        def xa_transposes(g):
-            if not 0 <= g < NG:
-                return
-            abank[g] = ps2.tile([P, 2 * TPG * P], BF16, name="abank", tag="misc")
-            for i in range(2 * TPG):
+        def b_transposes(k):
+            half = 0 if k == 1 else 1
+            bbank[k] = ps1.tile([P, F], BF16, name="bbank", tag="l%d" % k)
+            for c in range(4):
+                i = 4 * half + c
                 nc.tensor.transpose(
-                    abank[g][:, P * i : P * (i + 1)], xa_sb[g][:, R * i : R * (i + 1)], ident_b[:]
+                    bbank[k][:, P * c : P * (c + 1)], b_sb[:, R * i : R * (i + 1)], ident_b[:]
                 )
 
-        def xa_copy(g, copy):
-            if not 0 <= g < NG:
-                return
-            copy(out=xaT[g][:], in_=abank[g][:])
+        def b_copy(k, copy):
+            bT[k] = keep.tile([P, F], BF16, name="bT%d" % k)
+            copy(out=bT[k][:], in_=bbank[k][:])
 
-        w_transposes(1, ("mx1", "mx3"))
-        x_transposes(0, 0)
-        x_transposes(0, 1)
-        w_transposes(3, ("l1", "l3"))
-        w_copy(1, 0, nc.scalar.copy)
-        w_copy(1, 1, nc.vector.tensor_copy)
-        x_copy(0, 0, nc.scalar.copy)
-        x_copy(0, 1, nc.vector.tensor_copy)
-        w_quant(1)
-        w_copy(3, 0, nc.scalar.copy)
-        w_copy(3, 1, nc.vector.tensor_copy)
-        x_quant(0)
-        xa_transposes(0)
-        xa_copy(0, nc.scalar.copy)
-        bbank = ps1.tile([P, 2 * F], BF16, name="bbank", tag="gt")
-        for i in range(8):
-            nc.tensor.transpose(bbank[:, P * i : P * (i + 1)], b_sb[:, R * i : R * (i + 1)], ident_b[:])
-        bT = keep.tile([P, 2 * F], BF16, name="bT")
-        nc.scalar.copy(out=bT[:], in_=bbank[:])
-        w_quant(3)
-        a2bank = ps1.tile([P, 4, P], BF16, name="a2bank", tag="o")
-        for c in range(4):
-            nc.tensor.transpose(a2bank[:, c, :], a_sb[:, P * c : P * (c + 1)], ident_b[:])
         ag = keep.tile([P, 4 * R], BF16, name="ag", align_bytes=64)
         ac = keep.tile([P, R], U32, name="ac", align_bytes=64)
         asc = keep.tile([P, R], U8, name="asc", align_bytes=64)
+        a2bank = {}
+
+        def a2_transposes():
+            a2bank[0] = ps2.tile([P, 4, P], BF16, name="a2bank", tag="gt")
+            for c in range(4):
+                nc.tensor.transpose(a2bank[0][:, c, :], a_sb[:, P * c : P * (c + 1)], ident_b[:])
 
         def a2_copy():
             nc.vector.tensor_copy(
                 out=ag[:].rearrange("p (r c) -> p r c", c=4),
-                in_=a2bank[:].rearrange("p c r -> p r c"),
+                in_=a2bank[0][:].rearrange("p c r -> p r c"),
             )
 
         def a2_quant():
             nc.vector.quantize_mx(out=ac[:].bitcast(FP8X4), scales=asc[:], in_=ag[:])
+
+        xg = {}
+        xc = {}
+        xs = {}
+        xaT = {}
+        xbank = {}
+        abank = {}
+        for q in range(NP):
+            xc[q] = keep.tile([P, 2 * P], U32, name="xc%d" % q, align_bytes=64)
+            xs[q] = keep.tile([P, 2 * P], U8, name="xs%d" % q, align_bytes=64)
+            xaT[q] = keep.tile([P, 4 * P], BF16, name="xaT%d" % q)
+
+        def x_transposes(q):
+            if not okp(q):
+                return
+            g, h = divmod(q, 2)
+            xbank[q] = ps2.tile([P, 2, 2, P], F32, name="xbank", tag="misc")
+            word_transposes(x_sb[g][:].bitcast(F32)[:, 512 * h : 512 * h + 512], xbank[q])
+
+        def x_copy(q, copy):
+            if not okp(q):
+                return
+            xg[q] = rot3.tile([P, 8 * P], BF16, name="xg", tag="xg", align_bytes=64)
+            word_copy(copy, xg[q][:].bitcast(F32), xbank[q])
+
+        def x_quant(q):
+            if not okp(q):
+                return
+            nc.vector.quantize_mx(out=xc[q][:].bitcast(FP8X4), scales=xs[q][:], in_=xg[q][:])
+
+        def xa_transposes(q):
+            if not okp(q):
+                return
+            g, h = divmod(q, 2)
+            abank[q] = ps2.tile([P, 4 * P], BF16, name="abank", tag="misc")
+            for half in range(2):
+                for i in range(2):
+                    src = 4 * half + 2 * h + i
+                    dst = 2 * half + i
+                    nc.tensor.transpose(
+                        abank[q][:, P * dst : P * (dst + 1)],
+                        xa_sb[g][:, R * src : R * (src + 1)],
+                        ident_b[:],
+                    )
+
+        def xa_copy(q, copy):
+            if not okp(q):
+                return
+            copy(out=xaT[q][:], in_=abank[q][:])
 
         mx = {}
         lo = {}
@@ -210,18 +227,15 @@ def tile_feedforward_pa_t_kernel(
         gs = {}
         obank = {}
 
-        def ok(t):
-            return 0 <= t < NT
-
         def mx_pass(k, t):
             if not ok(t):
                 return
-            g, j = divmod(t, TPG)
+            q, i = divmod(t, 2)
             mx[(k, t)] = ps1.tile([P, F], F32, name="mx%d" % k, tag="mx%d" % k)
             nc.tensor.matmul_mx(
                 out=mx[(k, t)][:],
-                lhsT=xc[g][:, P * j : P * (j + 1)].bitcast(FP8X4),
-                lhsT_scale=xs[g][:, P * j : P * (j + 1)],
+                lhsT=xc[q][:, P * i : P * (i + 1)].bitcast(FP8X4),
+                lhsT_scale=xs[q][:, P * i : P * (i + 1)],
                 rhs=wc[k][:].bitcast(FP8X4),
                 rhs_scale=ws[k][:],
                 start=True,
@@ -231,14 +245,13 @@ def tile_feedforward_pa_t_kernel(
         def lora(k, t):
             if not ok(t):
                 return
-            g, j = divmod(t, TPG)
-            half = 0 if k == 1 else 1
-            i = TPG * half + j
+            q, i = divmod(t, 2)
+            col = (0 if k == 1 else 2) + i
             lo[(k, t)] = ps1.tile([P, F], F32, name="l%d" % k, tag="l%d" % k)
             nc.tensor.matmul(
                 out=lo[(k, t)][:],
-                lhsT=xaT[g][:, P * i : P * (i + 1)],
-                rhs=bT[:, F * half : F * (half + 1)],
+                lhsT=xaT[q][:, P * col : P * (col + 1)],
+                rhs=bT[k][:],
                 start=True,
                 stop=True,
             )
@@ -271,102 +284,166 @@ def tile_feedforward_pa_t_kernel(
         def gate(t):
             if not ok(t):
                 return
-            g, j = divmod(t, TPG)
-            if j == 0:
-                g_sb[g] = rot3.tile([P, TPG * F], F32, name="g_sb", tag="g_sb")
+            q, i = divmod(t, 2)
+            if i == 0:
+                g_sb[q] = rot6.tile([P, 2 * F], F32, name="g_sb", tag="g_sb")
+            cut = F // 2 if t == NT - 1 else F
             nc.gpsimd.tensor_tensor(
-                out=g_sb[g][:, F * j : F * (j + 1)], in0=s_sb[t][:], in1=h_sb[(3, t)][:], op=ALU.mult
+                out=g_sb[q][:, F * i : F * i + cut],
+                in0=s_sb[t][:, 0:cut],
+                in1=h_sb[(3, t)][:, 0:cut],
+                op=ALU.mult,
             )
-            if j % 2 == 1:
-                nc.sync.dma_start(
-                    out=gv[:, F * (t - 1) : F * (t + 1)], in_=g_sb[g][:, F * (j - 1) : F * (j + 1)]
+            if cut < F:
+                nc.vector.tensor_tensor(
+                    out=g_sb[q][:, F * i + cut : F * (i + 1)],
+                    in0=s_sb[t][:, cut:F],
+                    in1=h_sb[(3, t)][:, cut:F],
+                    op=ALU.mult,
                 )
+            if i == 1:
+                nc.sync.dma_start(out=gv[:, 2 * F * q : 2 * F * (q + 1)], in_=g_sb[q][:])
 
-        def g_transposes(t):
+        def g_transposes(q):
+            if not okp(q):
+                return
+            for i in range(2):
+                t = 2 * q + i
+                gbank[t] = ps2.tile([P, 4, P], F32, name="gbank", tag="gt")
+                for c in range(4):
+                    c0 = F * i + P * c
+                    nc.tensor.transpose(gbank[t][:, c, :], g_sb[q][:, c0 : c0 + P], ident_f[:])
+
+        def g_copy(t, copy):
             if not ok(t):
                 return
-            g, j = divmod(t, TPG)
-            gbank[t] = ps1.tile([P, 4, P], F32, name="gbank", tag="gt")
-            for c in range(4):
-                c0 = F * j + P * c
-                nc.tensor.transpose(gbank[t][:, c, :], g_sb[g][:, c0 : c0 + P], ident_f[:])
-
-        def g_copy(t):
-            if not ok(t):
-                return
-            gg[t] = rot3.tile([P, 4 * P], BF16, name="gg", tag="gg", align_bytes=64)
-            nc.vector.tensor_copy(
-                out=gg[t][:].rearrange("p (r c) -> p r c", c=4),
+            q, i = divmod(t, 2)
+            if i == 0:
+                gg[q] = rot3.tile([P, 8 * P], BF16, name="gg", tag="gg", align_bytes=64)
+            copy(
+                out=gg[q][:, 4 * P * i : 4 * P * (i + 1)].rearrange("p (r c) -> p r c", c=4),
                 in_=gbank[t][:].rearrange("p c r -> p r c"),
             )
 
-        def g_quant(t):
-            if not ok(t):
+        def g_quant(q):
+            if not okp(q):
                 return
-            gc[t] = rot3.tile([P, P], U32, name="gc", tag="gc", align_bytes=64)
-            gs[t] = rot3.tile([P, P], U8, name="gs", tag="gs", align_bytes=64)
-            nc.vector.quantize_mx(out=gc[t][:].bitcast(FP8X4), scales=gs[t][:], in_=gg[t][:])
+            gc[q] = rot3.tile([P, 2 * P], U32, name="gc", tag="gc", align_bytes=64)
+            gs[q] = rot3.tile([P, 2 * P], U8, name="gs", tag="gs", align_bytes=64)
+            nc.vector.quantize_mx(out=gc[q][:].bitcast(FP8X4), scales=gs[q][:], in_=gg[q][:])
 
-        def ga2(t):
-            if not ok(t):
+        def ga2(q):
+            if not okp(q):
                 return
-            g, j = divmod(t, TPG)
-            if j == 0:
-                obank[g] = ps1.tile([P, TPG, R], F32, name="obank", tag="o")
-            nc.tensor.matmul_mx(
-                out=obank[g][:, j, :],
-                lhsT=gc[t][:].bitcast(FP8X4),
-                lhsT_scale=gs[t][:],
-                rhs=ac[:].bitcast(FP8X4),
-                rhs_scale=asc[:],
-                start=True,
-                stop=True,
-            )
+            obank[q] = ps2.tile([P, 2, R], F32, name="obank", tag="misc")
+            for i in range(2):
+                nc.tensor.matmul_mx(
+                    out=obank[q][:, i, :],
+                    lhsT=gc[q][:, P * i : P * (i + 1)].bitcast(FP8X4),
+                    lhsT_scale=gs[q][:, P * i : P * (i + 1)],
+                    rhs=ac[:].bitcast(FP8X4),
+                    rhs_scale=asc[:],
+                    start=True,
+                    stop=True,
+                )
 
-        def o_out(g):
-            if not 0 <= g < NG:
+        def o_out(q):
+            if not okp(q):
                 return
-            o_sb = rot2.tile([P, TPG * R], F32, name="o_sb", tag="o_sb")
-            nc.scalar.copy(out=o_sb[:], in_=obank[g][:].rearrange("p j r -> p (j r)"))
-            nc.sync.dma_start(out=ov[:, TPG * R * g : TPG * R * (g + 1)], in_=o_sb[:])
+            o_sb = rot3.tile([P, 2 * R], F32, name="o_sb", tag="o_sb")
+            nc.scalar.copy(out=o_sb[:], in_=obank[q][:].rearrange("p j r -> p (j r)"))
+            nc.sync.dma_start(out=ov[:, 2 * R * q : 2 * R * (q + 1)], in_=o_sb[:])
 
-        for t in range(-2, NT + 3):
-            g, r = divmod(t, TPG)
+        vcopy = nc.vector.tensor_copy
+        scopy = nc.scalar.copy
+
+        if WARM:
+            warm = keep.tile([P, F], BF16, name="warm")
+            nc.vector.memset(warm[:], 0.0)
+            wps = ps1.tile([P, F], F32, name="wps", tag="mx3")
+            for i in range(WARM):
+                nc.tensor.matmul(out=wps[:], lhsT=warm[:, 0:P], rhs=warm[:], start=True, stop=True)
+
+        w_transposes(1, 0)
+        w_transposes(1, 1)
+        w_copy(1, 0, scopy)
+        w_copy(1, 1, vcopy)
+        x_transposes(0)
+        x_copy(0, scopy)
+        w_quant(1)
+        xa_transposes(0)
+        xa_copy(0, vcopy)
+        w_transposes(3, 0)
+        w_transposes(3, 1)
+        x_quant(0)
+        w_copy(3, 0, vcopy)
+        w_copy(3, 1, vcopy)
+        mx_pass(1, 0)
+        b_transposes(1)
+        b_transposes(3)
+        b_copy(1, scopy)
+        mx_out(1, 0)
+        b_copy(3, scopy)
+        w_quant(3)
+        lora(1, 0)
+        mx_pass(1, 1)
+        x_transposes(1)
+        xa_transposes(1)
+        x_copy(1, scopy)
+        xa_copy(1, vcopy)
+        x_quant(1)
+        mx_pass(3, 0)
+        lora(3, 0)
+        mx_out(3, 0)
+        mx_pass(3, 1)
+        x_transposes(2)
+        xa_transposes(2)
+        x_copy(2, scopy)
+
+        for t in range(NT):
+            odd = t % 2 == 1
             mx_out(1, t + 1)
             add(1, t)
-            g_transposes(t - 2)
-            if r == 3 and t > 0:
-                x_transposes(g + 2, 0)
-            if r == 0:
-                if t == 0:
-                    x_transposes(1, 0)
-                x_transposes(g + 1, 1)
-            if r == 1 and t > 0:
-                xa_transposes(g + 1)
+            if odd:
+                g_transposes((t - 3) // 2)
+                x_transposes((t + 5) // 2)
+                xa_transposes((t + 5) // 2)
+                if t == 1:
+                    a2_transposes()
             lora(1, t + 1)
             mx_pass(1, t + 2)
             mx_out(3, t + 1)
             mx_pass(3, t + 2)
+            if odd:
+                g_quant((t - 5) // 2)
+                x_quant((t + 3) // 2)
+                if t == 3:
+                    a2_quant()
             add(3, t)
-            g_quant(t - 3)
-            ga2(t - 3)
+            if not odd:
+                ga2((t - 6) // 2)
             lora(3, t + 1)
-            if t == -1:
-                a2_copy()
-            if t == 0:
-                a2_quant()
-            if r == 1 and t > 0:
-                x_quant(g + 1)
-            if r == 2 and t > 0:
-                xa_copy(g + 1, nc.vector.tensor_copy)
             silu(t)
-            if r == 3 and t > 0:
-                x_copy(g + 2, 0, nc.scalar.copy)
-            if r == 0:
-                if t == 0:
-                    x_copy(1, 0, nc.scalar.copy)
-                x_copy(g + 1, 1, nc.scalar.copy)
-            if r == 2:
-                o_out(g - 1)
+            if odd:
+                x_copy((t + 5) // 2, scopy)
+            else:
+                o_out((t - 6) // 2)
             gate(t)
-            g_copy(t - 2)
+            g_copy(t - 3, vcopy)
+            if not odd:
+                xa_copy((t + 4) // 2, vcopy)
+            if t == 1:
+                a2_copy()
+
+        g_copy(NT - 3, scopy)
+        ga2(NP - 3)
+        o_out(NP - 3)
+        g_transposes(NP - 1)
+        g_quant(NP - 2)
+        g_copy(NT - 2, scopy)
+        g_copy(NT - 1, vcopy)
+        ga2(NP - 2)
+        o_out(NP - 2)
+        g_quant(NP - 1)
+        ga2(NP - 1)
+        o_out(NP - 1)

@@ -17,8 +17,8 @@ D = 512
 F = 512
 R = 128
 NT = TOKENS // P
-NP = NT // 2
-NG = NT // 4
+TPG = 4
+NG = NT // TPG
 WARM = 5
 FLOPS = 2 * TOKENS * (2 * D * F + 2 * R * F + F * R)
 
@@ -36,8 +36,8 @@ def tile_feedforward_pa_t_kernel(
     with ExitStack() as ctx:
         ctx.enter_context(tc.manual_schedule())
         keep = ctx.enter_context(tc.tile_pool(name="keep", bufs=1))
+        rot2 = ctx.enter_context(tc.tile_pool(name="rot2", bufs=2))
         rot3 = ctx.enter_context(tc.tile_pool(name="rot3", bufs=3))
-        rot6 = ctx.enter_context(tc.tile_pool(name="rot6", bufs=6))
         ps1 = ctx.enter_context(tc.psum_pool(name="ps1", bufs=1))
         ps2 = ctx.enter_context(tc.psum_pool(name="ps2", bufs=2))
 
@@ -49,44 +49,42 @@ def tile_feedforward_pa_t_kernel(
         x_sb = {}
         xa_sb = {}
         for g in range(NG):
-            x_sb[g] = keep.tile([P, 4 * D], BF16, name="x_sb%d" % g)
-            xa_sb[g] = keep.tile([P, 2 * 4 * R], BF16, name="xa_sb%d" % g)
+            x_sb[g] = keep.tile([P, TPG * D], BF16, name="x_sb%d" % g)
+            xa_sb[g] = keep.tile([P, 2 * TPG * R], BF16, name="xa_sb%d" % g)
 
-        def load_w(k, w, h):
-            nc.sync.dma_start(
-                out=w_sb[k][:, 2 * D * h : 2 * D * (h + 1)].rearrange("p (c d) -> p c d", c=2),
-                in_=w[2 * P * h : 2 * P * (h + 1), :].rearrange("(c p) d -> p c d", p=P),
-            )
+        def load_w(k, w):
+            for h in range(2):
+                nc.sync.dma_start(
+                    out=w_sb[k][:, 2 * D * h : 2 * D * (h + 1)].rearrange("p (c d) -> p c d", c=2),
+                    in_=w[2 * P * h : 2 * P * (h + 1), :].rearrange("(c p) d -> p c d", p=P),
+                )
 
-        def load_x(c0, c1):
-            g = c0 // (4 * D)
-            nc.sync.dma_start(out=x_sb[g][:, c0 - 4 * D * g : c1 - 4 * D * g], in_=xv[:, c0:c1])
+        def load_x(g):
+            nc.sync.dma_start(out=x_sb[g][:], in_=xv[:, TPG * D * g : TPG * D * (g + 1)])
 
         def load_xa(g):
-            n = 4 * R
+            n = TPG * R
             nc.sync.dma_start(out=xa_sb[g][:, 0:n], in_=xa1v[:, n * g : n * (g + 1)])
             nc.sync.dma_start(out=xa_sb[g][:, n : 2 * n], in_=xa3v[:, n * g : n * (g + 1)])
 
-        def load_b(half, b):
-            nc.sync.dma_start(
-                out=b_sb[:, 4 * R * half : 4 * R * (half + 1)].rearrange("p (c r) -> p c r", c=4),
-                in_=b.rearrange("(c p) r -> p c r", p=P),
-            )
-
-        load_w(1, w1, 0)
-        load_w(1, w1, 1)
-        load_x(0, 2 * D)
+        load_w(1, w1)
+        nc.sync.dma_start(out=x_sb[0][:, 0 : 2 * D], in_=xv[:, 0 : 2 * D])
+        nc.sync.dma_start(out=x_sb[0][:, 2 * D : 4 * D], in_=xv[:, 2 * D : 4 * D])
+        load_w(3, w3)
         load_xa(0)
-        load_w(3, w3, 0)
-        load_w(3, w3, 1)
-        load_b(0, lora_B1)
-        load_b(1, lora_B3)
-        load_x(2 * D, 4 * D)
-        load_x(4 * D, 8 * D)
-        load_xa(1)
+        nc.sync.dma_start(
+            out=b_sb[:, 0 : 4 * R].rearrange("p (c r) -> p c r", c=4),
+            in_=lora_B1.rearrange("(c p) r -> p c r", p=P),
+        )
+        nc.sync.dma_start(
+            out=b_sb[:, 4 * R : 8 * R].rearrange("p (c r) -> p c r", c=4),
+            in_=lora_B3.rearrange("(c p) r -> p c r", p=P),
+        )
+        load_x(1)
         nc.sync.dma_start(out=a_sb[:], in_=lora_A2)
+        load_xa(1)
         for g in range(2, NG):
-            load_x(4 * D * g, 4 * D * (g + 1))
+            load_x(g)
             load_xa(g)
 
         ident_f = keep.tile([P, P], F32, name="ident_f")
@@ -106,12 +104,6 @@ def tile_feedforward_pa_t_kernel(
                 in_=bank[:].rearrange("p a u r -> p a r u"),
             )
 
-        def okp(q):
-            return 0 <= q < NP
-
-        def ok(t):
-            return 0 <= t < NT
-
         wg = {}
         wc = {}
         ws = {}
@@ -120,10 +112,21 @@ def tile_feedforward_pa_t_kernel(
             wg[k] = keep.tile([P, 4 * F], BF16, name="wg%d" % k, align_bytes=64)
             wc[k] = keep.tile([P, F], U32, name="wc%d" % k, align_bytes=64)
             ws[k] = keep.tile([P, F], U8, name="ws%d" % k, align_bytes=64)
+        xg = {}
+        xc = {}
+        xs = {}
+        xaT = {}
+        xbank = {}
+        abank = {}
+        for g in range(NG):
+            xc[g] = keep.tile([P, TPG * P], U32, name="xc%d" % g, align_bytes=64)
+            xs[g] = keep.tile([P, TPG * P], U8, name="xs%d" % g, align_bytes=64)
+            xaT[g] = keep.tile([P, 2 * TPG * P], BF16, name="xaT%d" % g)
 
-        def w_transposes(k, h):
-            wbank[(k, h)] = ps2.tile([P, 2, 2, P], F32, name="wbank", tag="gt")
-            word_transposes(w_sb[k][:].bitcast(F32)[:, 512 * h : 512 * h + 512], wbank[(k, h)])
+        def w_transposes(k, tags):
+            for h in range(2):
+                wbank[(k, h)] = ps1.tile([P, 2, 2, P], F32, name="wbank", tag=tags[h])
+                word_transposes(w_sb[k][:].bitcast(F32)[:, 512 * h : 512 * h + 512], wbank[(k, h)])
 
         def w_copy(k, h, copy):
             word_copy(copy, wg[k][:].bitcast(F32)[:, 512 * h : 512 * h + 512], wbank[(k, h)])
@@ -131,89 +134,78 @@ def tile_feedforward_pa_t_kernel(
         def w_quant(k):
             nc.vector.quantize_mx(out=wc[k][:].bitcast(FP8X4), scales=ws[k][:], in_=wg[k][:])
 
-        bT = {}
-        bbank = {}
+        def x_transposes(g, h):
+            if not 0 <= g < NG:
+                return
+            xbank[(g, h)] = ps2.tile([P, 2, 2, P], F32, name="xbank", tag="misc")
+            word_transposes(x_sb[g][:].bitcast(F32)[:, 512 * h : 512 * h + 512], xbank[(g, h)])
 
-        def b_transposes(k):
-            half = 0 if k == 1 else 1
-            bbank[k] = ps1.tile([P, F], BF16, name="bbank", tag="l%d" % k)
-            for c in range(4):
-                i = 4 * half + c
+        def x_copy(g, h, copy):
+            if not 0 <= g < NG:
+                return
+            if h == 0:
+                xg[g] = rot2.tile([P, 4 * TPG * P], BF16, name="xg", tag="xg", align_bytes=64)
+            word_copy(copy, xg[g][:].bitcast(F32)[:, 512 * h : 512 * h + 512], xbank[(g, h)])
+
+        def x_quant(g):
+            if not 0 <= g < NG:
+                return
+            nc.vector.quantize_mx(out=xc[g][:].bitcast(FP8X4), scales=xs[g][:], in_=xg[g][:])
+
+        def xa_transposes(g):
+            if not 0 <= g < NG:
+                return
+            abank[g] = ps2.tile([P, 2 * TPG * P], BF16, name="abank", tag="misc")
+            for i in range(2 * TPG):
                 nc.tensor.transpose(
-                    bbank[k][:, P * c : P * (c + 1)], b_sb[:, R * i : R * (i + 1)], ident_b[:]
+                    abank[g][:, P * i : P * (i + 1)], xa_sb[g][:, R * i : R * (i + 1)], ident_b[:]
                 )
 
-        def b_copy(k, copy):
-            bT[k] = keep.tile([P, F], BF16, name="bT%d" % k)
-            copy(out=bT[k][:], in_=bbank[k][:])
+        def xa_copy(g, copy):
+            if not 0 <= g < NG:
+                return
+            copy(out=xaT[g][:], in_=abank[g][:])
 
+        warm = keep.tile([P, F], BF16, name="warm")
+        nc.vector.memset(warm[:], 0.0)
+        wps = ps1.tile([P, F], F32, name="wps", tag="gt")
+        for i in range(WARM):
+            nc.tensor.matmul(out=wps[:], lhsT=warm[:, 0:P], rhs=warm[:], start=True, stop=True)
+        w_transposes(1, ("mx1", "mx3"))
+        x_transposes(0, 0)
+        x_transposes(0, 1)
+        w_transposes(3, ("l1", "l3"))
+        w_copy(1, 0, nc.scalar.copy)
+        w_copy(1, 1, nc.vector.tensor_copy)
+        x_copy(0, 0, nc.scalar.copy)
+        x_copy(0, 1, nc.vector.tensor_copy)
+        w_quant(1)
+        w_copy(3, 0, nc.scalar.copy)
+        w_copy(3, 1, nc.vector.tensor_copy)
+        x_quant(0)
+        xa_transposes(0)
+        xa_copy(0, nc.scalar.copy)
+        bbank = ps1.tile([P, 2 * F], BF16, name="bbank", tag="gt")
+        for i in range(8):
+            nc.tensor.transpose(bbank[:, P * i : P * (i + 1)], b_sb[:, R * i : R * (i + 1)], ident_b[:])
+        bT = keep.tile([P, 2 * F], BF16, name="bT")
+        nc.scalar.copy(out=bT[:], in_=bbank[:])
+        w_quant(3)
+        a2bank = ps1.tile([P, 4, P], BF16, name="a2bank", tag="o")
+        for c in range(4):
+            nc.tensor.transpose(a2bank[:, c, :], a_sb[:, P * c : P * (c + 1)], ident_b[:])
         ag = keep.tile([P, 4 * R], BF16, name="ag", align_bytes=64)
         ac = keep.tile([P, R], U32, name="ac", align_bytes=64)
         asc = keep.tile([P, R], U8, name="asc", align_bytes=64)
-        a2bank = {}
-
-        def a2_transposes():
-            a2bank[0] = ps2.tile([P, 4, P], BF16, name="a2bank", tag="gt")
-            for c in range(4):
-                nc.tensor.transpose(a2bank[0][:, c, :], a_sb[:, P * c : P * (c + 1)], ident_b[:])
 
         def a2_copy():
             nc.vector.tensor_copy(
                 out=ag[:].rearrange("p (r c) -> p r c", c=4),
-                in_=a2bank[0][:].rearrange("p c r -> p r c"),
+                in_=a2bank[:].rearrange("p c r -> p r c"),
             )
 
         def a2_quant():
             nc.vector.quantize_mx(out=ac[:].bitcast(FP8X4), scales=asc[:], in_=ag[:])
-
-        xg = {}
-        xc = {}
-        xs = {}
-        xaT = {}
-        xbank = {}
-        abank = {}
-        for q in range(NP):
-            xc[q] = keep.tile([P, 2 * P], U32, name="xc%d" % q, align_bytes=64)
-            xs[q] = keep.tile([P, 2 * P], U8, name="xs%d" % q, align_bytes=64)
-            xaT[q] = keep.tile([P, 4 * P], BF16, name="xaT%d" % q)
-
-        def x_transposes(q):
-            if not okp(q):
-                return
-            g, h = divmod(q, 2)
-            xbank[q] = ps2.tile([P, 2, 2, P], F32, name="xbank", tag="misc")
-            word_transposes(x_sb[g][:].bitcast(F32)[:, 512 * h : 512 * h + 512], xbank[q])
-
-        def x_copy(q, copy):
-            if not okp(q):
-                return
-            xg[q] = rot3.tile([P, 8 * P], BF16, name="xg", tag="xg", align_bytes=64)
-            word_copy(copy, xg[q][:].bitcast(F32), xbank[q])
-
-        def x_quant(q):
-            if not okp(q):
-                return
-            nc.vector.quantize_mx(out=xc[q][:].bitcast(FP8X4), scales=xs[q][:], in_=xg[q][:])
-
-        def xa_transposes(q):
-            if not okp(q):
-                return
-            g, h = divmod(q, 2)
-            abank[q] = ps2.tile([P, 4 * P], BF16, name="abank", tag="misc")
-            for half in range(2):
-                for i in range(2):
-                    src = 4 * half + 2 * h + i
-                    dst = 2 * half + i
-                    nc.tensor.transpose(
-                        abank[q][:, P * dst : P * (dst + 1)],
-                        xa_sb[g][:, R * src : R * (src + 1)],
-                        ident_b[:],
-                    )
-
-        def xa_copy(q, copy):
-            if not okp(q):
-                return
-            copy(out=xaT[q][:], in_=abank[q][:])
 
         mx = {}
         lo = {}
@@ -227,15 +219,18 @@ def tile_feedforward_pa_t_kernel(
         gs = {}
         obank = {}
 
+        def ok(t):
+            return 0 <= t < NT
+
         def mx_pass(k, t):
             if not ok(t):
                 return
-            q, i = divmod(t, 2)
+            g, j = divmod(t, TPG)
             mx[(k, t)] = ps1.tile([P, F], F32, name="mx%d" % k, tag="mx%d" % k)
             nc.tensor.matmul_mx(
                 out=mx[(k, t)][:],
-                lhsT=xc[q][:, P * i : P * (i + 1)].bitcast(FP8X4),
-                lhsT_scale=xs[q][:, P * i : P * (i + 1)],
+                lhsT=xc[g][:, P * j : P * (j + 1)].bitcast(FP8X4),
+                lhsT_scale=xs[g][:, P * j : P * (j + 1)],
                 rhs=wc[k][:].bitcast(FP8X4),
                 rhs_scale=ws[k][:],
                 start=True,
@@ -245,13 +240,14 @@ def tile_feedforward_pa_t_kernel(
         def lora(k, t):
             if not ok(t):
                 return
-            q, i = divmod(t, 2)
-            col = (0 if k == 1 else 2) + i
+            g, j = divmod(t, TPG)
+            half = 0 if k == 1 else 1
+            i = TPG * half + j
             lo[(k, t)] = ps1.tile([P, F], F32, name="l%d" % k, tag="l%d" % k)
             nc.tensor.matmul(
                 out=lo[(k, t)][:],
-                lhsT=xaT[q][:, P * col : P * (col + 1)],
-                rhs=bT[k][:],
+                lhsT=xaT[g][:, P * i : P * (i + 1)],
+                rhs=bT[:, F * half : F * (half + 1)],
                 start=True,
                 stop=True,
             )
@@ -284,166 +280,117 @@ def tile_feedforward_pa_t_kernel(
         def gate(t):
             if not ok(t):
                 return
-            q, i = divmod(t, 2)
-            if i == 0:
-                g_sb[q] = rot6.tile([P, 2 * F], F32, name="g_sb", tag="g_sb")
+            g, j = divmod(t, TPG)
+            if j == 0:
+                g_sb[g] = rot3.tile([P, TPG * F], F32, name="g_sb", tag="g_sb")
             cut = F // 2 if t == NT - 1 else F
             nc.gpsimd.tensor_tensor(
-                out=g_sb[q][:, F * i : F * i + cut],
+                out=g_sb[g][:, F * j : F * j + cut],
                 in0=s_sb[t][:, 0:cut],
                 in1=h_sb[(3, t)][:, 0:cut],
                 op=ALU.mult,
             )
             if cut < F:
                 nc.vector.tensor_tensor(
-                    out=g_sb[q][:, F * i + cut : F * (i + 1)],
+                    out=g_sb[g][:, F * j + cut : F * (j + 1)],
                     in0=s_sb[t][:, cut:F],
                     in1=h_sb[(3, t)][:, cut:F],
                     op=ALU.mult,
                 )
-            if i == 1:
-                nc.sync.dma_start(out=gv[:, 2 * F * q : 2 * F * (q + 1)], in_=g_sb[q][:])
+            if j % 2 == 1:
+                nc.sync.dma_start(
+                    out=gv[:, F * (t - 1) : F * (t + 1)], in_=g_sb[g][:, F * (j - 1) : F * (j + 1)]
+                )
 
-        def g_transposes(q):
-            if not okp(q):
-                return
-            for i in range(2):
-                t = 2 * q + i
-                gbank[t] = ps2.tile([P, 4, P], F32, name="gbank", tag="gt")
-                for c in range(4):
-                    c0 = F * i + P * c
-                    nc.tensor.transpose(gbank[t][:, c, :], g_sb[q][:, c0 : c0 + P], ident_f[:])
-
-        def g_copy(t, copy):
+        def g_transposes(t):
             if not ok(t):
                 return
-            q, i = divmod(t, 2)
-            if i == 0:
-                gg[q] = rot3.tile([P, 8 * P], BF16, name="gg", tag="gg", align_bytes=64)
-            copy(
-                out=gg[q][:, 4 * P * i : 4 * P * (i + 1)].rearrange("p (r c) -> p r c", c=4),
+            g, j = divmod(t, TPG)
+            gbank[t] = ps1.tile([P, 4, P], F32, name="gbank", tag="gt")
+            for c in range(4):
+                c0 = F * j + P * c
+                nc.tensor.transpose(gbank[t][:, c, :], g_sb[g][:, c0 : c0 + P], ident_f[:])
+
+        def g_copy(t):
+            if not ok(t):
+                return
+            gg[t] = rot3.tile([P, 4 * P], BF16, name="gg", tag="gg", align_bytes=64)
+            nc.vector.tensor_copy(
+                out=gg[t][:].rearrange("p (r c) -> p r c", c=4),
                 in_=gbank[t][:].rearrange("p c r -> p r c"),
             )
 
-        def g_quant(q):
-            if not okp(q):
+        def g_quant(t):
+            if not ok(t):
                 return
-            gc[q] = rot3.tile([P, 2 * P], U32, name="gc", tag="gc", align_bytes=64)
-            gs[q] = rot3.tile([P, 2 * P], U8, name="gs", tag="gs", align_bytes=64)
-            nc.vector.quantize_mx(out=gc[q][:].bitcast(FP8X4), scales=gs[q][:], in_=gg[q][:])
+            gc[t] = rot3.tile([P, P], U32, name="gc", tag="gc", align_bytes=64)
+            gs[t] = rot3.tile([P, P], U8, name="gs", tag="gs", align_bytes=64)
+            nc.vector.quantize_mx(out=gc[t][:].bitcast(FP8X4), scales=gs[t][:], in_=gg[t][:])
 
-        def ga2(q):
-            if not okp(q):
+        def ga2(t):
+            if not ok(t):
                 return
-            obank[q] = ps2.tile([P, 2, R], F32, name="obank", tag="misc")
-            for i in range(2):
-                nc.tensor.matmul_mx(
-                    out=obank[q][:, i, :],
-                    lhsT=gc[q][:, P * i : P * (i + 1)].bitcast(FP8X4),
-                    lhsT_scale=gs[q][:, P * i : P * (i + 1)],
-                    rhs=ac[:].bitcast(FP8X4),
-                    rhs_scale=asc[:],
-                    start=True,
-                    stop=True,
-                )
+            g, j = divmod(t, TPG)
+            if j == 0:
+                obank[g] = ps1.tile([P, TPG, R], F32, name="obank", tag="o")
+            nc.tensor.matmul_mx(
+                out=obank[g][:, j, :],
+                lhsT=gc[t][:].bitcast(FP8X4),
+                lhsT_scale=gs[t][:],
+                rhs=ac[:].bitcast(FP8X4),
+                rhs_scale=asc[:],
+                start=True,
+                stop=True,
+            )
 
-        def o_out(q):
-            if not okp(q):
+        def o_out(g, j0, j1):
+            if not 0 <= g < NG:
                 return
-            o_sb = rot3.tile([P, 2 * R], F32, name="o_sb", tag="o_sb")
-            nc.scalar.copy(out=o_sb[:], in_=obank[q][:].rearrange("p j r -> p (j r)"))
-            nc.sync.dma_start(out=ov[:, 2 * R * q : 2 * R * (q + 1)], in_=o_sb[:])
+            o_sb = rot2.tile([P, (j1 - j0) * R], F32, name="o_sb", tag="o_sb%d" % (j1 - j0))
+            nc.scalar.copy(out=o_sb[:], in_=obank[g][:, j0:j1, :].rearrange("p j r -> p (j r)"))
+            nc.sync.dma_start(out=ov[:, R * (TPG * g + j0) : R * (TPG * g + j1)], in_=o_sb[:])
 
-        vcopy = nc.vector.tensor_copy
-        scopy = nc.scalar.copy
-
-        if WARM:
-            warm = keep.tile([P, F], BF16, name="warm")
-            nc.vector.memset(warm[:], 0.0)
-            wps = ps1.tile([P, F], F32, name="wps", tag="mx3")
-            for i in range(WARM):
-                nc.tensor.matmul(out=wps[:], lhsT=warm[:, 0:P], rhs=warm[:], start=True, stop=True)
-
-        w_transposes(1, 0)
-        w_transposes(1, 1)
-        w_copy(1, 0, scopy)
-        w_copy(1, 1, vcopy)
-        x_transposes(0)
-        x_copy(0, scopy)
-        w_quant(1)
-        xa_transposes(0)
-        xa_copy(0, vcopy)
-        w_transposes(3, 0)
-        w_transposes(3, 1)
-        x_quant(0)
-        w_copy(3, 0, vcopy)
-        w_copy(3, 1, vcopy)
-        mx_pass(1, 0)
-        b_transposes(1)
-        b_transposes(3)
-        b_copy(1, scopy)
-        mx_out(1, 0)
-        b_copy(3, scopy)
-        w_quant(3)
-        lora(1, 0)
-        mx_pass(1, 1)
-        x_transposes(1)
-        xa_transposes(1)
-        x_copy(1, scopy)
-        xa_copy(1, vcopy)
-        x_quant(1)
-        mx_pass(3, 0)
-        lora(3, 0)
-        mx_out(3, 0)
-        mx_pass(3, 1)
-        x_transposes(2)
-        xa_transposes(2)
-        x_copy(2, scopy)
-
-        for t in range(NT):
-            odd = t % 2 == 1
-            mx_out(1, t + 1)
+        for t in range(-2, NT + 3):
+            g, r = divmod(t, TPG)
             add(1, t)
-            if odd:
-                g_transposes((t - 3) // 2)
-                x_transposes((t + 5) // 2)
-                xa_transposes((t + 5) // 2)
-                if t == 1:
-                    a2_transposes()
+            if r == 2 and t > 0:
+                xa_copy(g + 1, nc.scalar.copy)
+            mx_out(1, t + 1)
+            if r == 1 and t > 0:
+                xa_transposes(g + 1)
+            if r == 0:
+                x_transposes(g + 1, 1)
+            mx_out(3, t + 1)
+            add(3, t)
+            g_quant(t - 3)
+            if t == -1:
+                a2_copy()
+            if t == 0:
+                a2_quant()
+            if r == 1 and t > 0:
+                x_quant(g + 1)
+            gate(t - 1)
+            g_transposes(t - 2)
+            if r == 3 and t > 0:
+                x_transposes(g + 2, 0)
+            if t == 0:
+                x_transposes(1, 0)
+            g_copy(t - 2)
+            if t == 0:
+                x_copy(1, 0, nc.vector.tensor_copy)
+            silu(t)
+            if r == 0:
+                x_copy(g + 1, 1, nc.scalar.copy)
             lora(1, t + 1)
             mx_pass(1, t + 2)
-            mx_out(3, t + 1)
+            ga2(t - 3)
+            if r == 2 and g < NG:
+                o_out(g - 1, 0, TPG)
+            if t == NT + 1:
+                o_out(NG - 1, 0, TPG - 1)
+            if t == NT + 2:
+                o_out(NG - 1, TPG - 1, TPG)
             mx_pass(3, t + 2)
-            if odd:
-                g_quant((t - 5) // 2)
-                x_quant((t + 3) // 2)
-                if t == 3:
-                    a2_quant()
-            add(3, t)
-            if not odd:
-                ga2((t - 6) // 2)
             lora(3, t + 1)
-            silu(t)
-            if odd:
-                x_copy((t + 5) // 2, scopy)
-            else:
-                o_out((t - 6) // 2)
-            gate(t)
-            g_copy(t - 3, vcopy)
-            if not odd:
-                xa_copy((t + 4) // 2, vcopy)
-            if t == 1:
-                a2_copy()
-
-        g_copy(NT - 3, scopy)
-        ga2(NP - 3)
-        o_out(NP - 3)
-        g_transposes(NP - 1)
-        g_quant(NP - 2)
-        g_copy(NT - 2, scopy)
-        g_copy(NT - 1, vcopy)
-        ga2(NP - 2)
-        o_out(NP - 2)
-        g_quant(NP - 1)
-        ga2(NP - 1)
-        o_out(NP - 1)
+            if r == 3 and t > 0:
+                x_copy(g + 2, 0, nc.vector.tensor_copy)

@@ -352,45 +352,43 @@ def tile_feedforward_pa_t_kernel(
 
         for t in range(-2, NT + 3):
             g, r = divmod(t, TPG)
-            add(1, t)
-            if r == 2 and t > 0:
-                xa_copy(g + 1, nc.scalar.copy)
             mx_out(1, t + 1)
-            if r == 1 and t > 0:
-                xa_transposes(g + 1)
+            g_transposes(t - 2)
+            add(1, t)
+            if t == -1:
+                x_transposes(1, 0)
+            if r == 3:
+                x_transposes(g + 2, 1)
+            if r == 1:
+                x_transposes(g + 2, 0)
             if r == 0:
-                x_transposes(g + 1, 1)
-            mx_out(3, t + 1)
+                xa_transposes(g + 1)
+            lora(1, t + 1)
+            silu(t)
             add(3, t)
             g_quant(t - 3)
+            mx_out(3, t + 1)
+            if r == 3:
+                x_copy(g + 2, 0, nc.scalar.copy)
+            gate(t - 1)
+            if r == 1:
+                x_quant(g + 1)
             if t == -1:
                 a2_copy()
             if t == 0:
                 a2_quant()
-            if r == 1 and t > 0:
-                x_quant(g + 1)
-            gate(t - 1)
-            g_transposes(t - 2)
-            if r == 3 and t > 0:
-                x_transposes(g + 2, 0)
-            if t == 0:
-                x_transposes(1, 0)
-            g_copy(t - 2)
-            if t == 0:
-                x_copy(1, 0, nc.vector.tensor_copy)
-            silu(t)
-            if r == 0:
-                x_copy(g + 1, 1, nc.scalar.copy)
-            lora(1, t + 1)
             mx_pass(1, t + 2)
             ga2(t - 3)
+            if r == 1:
+                xa_copy(g + 1, nc.scalar.copy)
+            lora(3, t + 1)
             if r == 2 and g < NG:
                 o_out(g - 1, 0, TPG)
             if t == NT + 1:
                 o_out(NG - 1, 0, TPG - 1)
             if t == NT + 2:
                 o_out(NG - 1, TPG - 1, TPG)
+            if r == 0:
+                x_copy(g + 1, 1, nc.scalar.copy)
+            g_copy(t - 2)
             mx_pass(3, t + 2)
-            lora(3, t + 1)
-            if r == 3 and t > 0:
-                x_copy(g + 2, 0, nc.vector.tensor_copy)

@@ -20,6 +20,7 @@ NT = TOKENS // P
 TPG = 4
 NG = NT // TPG
 WARM = 5
+GCUT = F
 FLOPS = 2 * TOKENS * (2 * D * F + 2 * R * F + F * R)
 
 
@@ -69,7 +70,6 @@ def tile_feedforward_pa_t_kernel(
 
         load_w(1, w1)
         nc.sync.dma_start(out=x_sb[0][:, 0 : 2 * D], in_=xv[:, 0 : 2 * D])
-        nc.sync.dma_start(out=x_sb[0][:, 2 * D : 4 * D], in_=xv[:, 2 * D : 4 * D])
         load_w(3, w3)
         load_xa(0)
         nc.sync.dma_start(
@@ -80,9 +80,10 @@ def tile_feedforward_pa_t_kernel(
             out=b_sb[:, 4 * R : 8 * R].rearrange("p (c r) -> p c r", c=4),
             in_=lora_B3.rearrange("(c p) r -> p c r", p=P),
         )
+        nc.sync.dma_start(out=x_sb[0][:, 2 * D : 4 * D], in_=xv[:, 2 * D : 4 * D])
         load_x(1)
-        nc.sync.dma_start(out=a_sb[:], in_=lora_A2)
         load_xa(1)
+        nc.sync.dma_start(out=a_sb[:], in_=lora_A2)
         for g in range(2, NG):
             load_x(g)
             load_xa(g)
@@ -166,42 +167,37 @@ def tile_feedforward_pa_t_kernel(
                 return
             copy(out=xaT[g][:], in_=abank[g][:])
 
-        warm = keep.tile([P, F], BF16, name="warm")
-        nc.vector.memset(warm[:], 0.0)
-        wps = ps1.tile([P, F], F32, name="wps", tag="gt")
-        for i in range(WARM):
-            nc.tensor.matmul(out=wps[:], lhsT=warm[:, 0:P], rhs=warm[:], start=True, stop=True)
-        w_transposes(1, ("mx1", "mx3"))
-        x_transposes(0, 0)
-        x_transposes(0, 1)
-        w_transposes(3, ("l1", "l3"))
-        w_copy(1, 0, nc.scalar.copy)
-        w_copy(1, 1, nc.vector.tensor_copy)
-        x_copy(0, 0, nc.scalar.copy)
-        x_copy(0, 1, nc.vector.tensor_copy)
-        w_quant(1)
-        w_copy(3, 0, nc.scalar.copy)
-        w_copy(3, 1, nc.vector.tensor_copy)
-        x_quant(0)
-        xa_transposes(0)
-        xa_copy(0, nc.scalar.copy)
-        bbank = ps1.tile([P, 2 * F], BF16, name="bbank", tag="gt")
-        for i in range(8):
-            nc.tensor.transpose(bbank[:, P * i : P * (i + 1)], b_sb[:, R * i : R * (i + 1)], ident_b[:])
+        def x_quant_part(h):
+            nc.vector.quantize_mx(
+                out=xc[0][:, 2 * P * h : 2 * P * (h + 1)].bitcast(FP8X4),
+                scales=xs[0][:, 2 * P * h : 2 * P * (h + 1)],
+                in_=xg[0][:, 8 * P * h : 8 * P * (h + 1)],
+            )
+
         bT = keep.tile([P, 2 * F], BF16, name="bT")
-        nc.scalar.copy(out=bT[:], in_=bbank[:])
-        w_quant(3)
-        a2bank = ps1.tile([P, 4, P], BF16, name="a2bank", tag="o")
-        for c in range(4):
-            nc.tensor.transpose(a2bank[:, c, :], a_sb[:, P * c : P * (c + 1)], ident_b[:])
+        bbank = {}
+
+        def b_transposes():
+            bbank[0] = ps1.tile([P, 2 * F], BF16, name="bbank", tag="gt")
+            for i in range(8):
+                nc.tensor.transpose(
+                    bbank[0][:, P * i : P * (i + 1)], b_sb[:, R * i : R * (i + 1)], ident_b[:]
+                )
+
         ag = keep.tile([P, 4 * R], BF16, name="ag", align_bytes=64)
         ac = keep.tile([P, R], U32, name="ac", align_bytes=64)
         asc = keep.tile([P, R], U8, name="asc", align_bytes=64)
+        a2bank = {}
+
+        def a2_transposes():
+            a2bank[0] = ps1.tile([P, 4, P], BF16, name="a2bank", tag="o")
+            for c in range(4):
+                nc.tensor.transpose(a2bank[0][:, c, :], a_sb[:, P * c : P * (c + 1)], ident_b[:])
 
         def a2_copy():
             nc.vector.tensor_copy(
                 out=ag[:].rearrange("p (r c) -> p r c", c=4),
-                in_=a2bank[:].rearrange("p c r -> p r c"),
+                in_=a2bank[0][:].rearrange("p c r -> p r c"),
             )
 
         def a2_quant():
@@ -283,7 +279,7 @@ def tile_feedforward_pa_t_kernel(
             g, j = divmod(t, TPG)
             if j == 0:
                 g_sb[g] = rot3.tile([P, TPG * F], F32, name="g_sb", tag="g_sb")
-            cut = F // 2 if t == NT - 1 else F
+            cut = F // 2 if t == NT - 1 else GCUT
             nc.gpsimd.tensor_tensor(
                 out=g_sb[g][:, F * j : F * j + cut],
                 in0=s_sb[t][:, 0:cut],
@@ -350,37 +346,80 @@ def tile_feedforward_pa_t_kernel(
             nc.scalar.copy(out=o_sb[:], in_=obank[g][:, j0:j1, :].rearrange("p j r -> p (j r)"))
             nc.sync.dma_start(out=ov[:, R * (TPG * g + j0) : R * (TPG * g + j1)], in_=o_sb[:])
 
-        for t in range(-2, NT + 3):
+        vcopy = nc.vector.tensor_copy
+        scopy = nc.scalar.copy
+
+        warm = keep.tile([P, F], BF16, name="warm")
+        nc.vector.memset(warm[:], 0.0)
+        wps = ps1.tile([P, F], F32, name="wps", tag="gt")
+        for i in range(WARM):
+            nc.tensor.matmul(out=wps[:], lhsT=warm[:, 0:P], rhs=warm[:], start=True, stop=True)
+
+        w_transposes(1, ("mx1", "mx3"))
+        w_copy(1, 0, scopy)
+        w_copy(1, 1, vcopy)
+        x_transposes(0, 0)
+        x_copy(0, 0, scopy)
+        w_quant(1)
+        w_transposes(3, ("l1", "l3"))
+        x_quant_part(0)
+        w_copy(3, 0, scopy)
+        w_copy(3, 1, vcopy)
+        xa_transposes(0)
+        b_transposes()
+        x_transposes(0, 1)
+        xa_copy(0, scopy)
+        w_quant(3)
+        vcopy(out=bT[:], in_=bbank[0][:])
+        x_copy(0, 1, vcopy)
+        x_quant_part(1)
+        mx_pass(1, 0)
+        mx_pass(3, 0)
+        mx_out(1, 0)
+        mx_out(3, 0)
+        lora(1, 0)
+        lora(3, 0)
+        mx_pass(1, 1)
+        mx_pass(3, 1)
+
+        step = {}
+        early = {}
+        for g in range(1, NG):
+            early[max(TPG * g - 7, 2 * g - 2)] = g
+            for k in range(3):
+                step[max(TPG * g - 5, 0) + k] = (g, k)
+
+        for t in range(NT + 3):
             g, r = divmod(t, TPG)
+            xg_, xk = step.get(t, (NG, 3))
             mx_out(1, t + 1)
             g_transposes(t - 2)
             add(1, t)
-            if t == -1:
-                x_transposes(1, 0)
-            if r == 3:
-                x_transposes(g + 2, 1)
-            if r == 1:
-                x_transposes(g + 2, 0)
-            if r == 0:
-                xa_transposes(g + 1)
+            x_transposes(early.get(t, NG), 0)
+            if xk == 0:
+                x_transposes(xg_, 1)
+            if xk == 1:
+                xa_transposes(xg_)
+            if t == 1:
+                a2_transposes()
             lora(1, t + 1)
             silu(t)
             add(3, t)
             g_quant(t - 3)
             mx_out(3, t + 1)
-            if r == 3:
-                x_copy(g + 2, 0, nc.scalar.copy)
+            if xk == 0 and xg_ % 2 == 1:
+                x_copy(xg_, 0, scopy)
             gate(t - 1)
-            if r == 1:
-                x_quant(g + 1)
-            if t == -1:
-                a2_copy()
-            if t == 0:
+            if xk == 0 and xg_ % 2 == 0:
+                x_copy(xg_, 0, vcopy)
+            if xk == 2:
+                x_quant(xg_)
+            if t == 2:
                 a2_quant()
             mx_pass(1, t + 2)
             ga2(t - 3)
-            if r == 1:
-                xa_copy(g + 1, nc.scalar.copy)
+            if xk == 2:
+                xa_copy(xg_, scopy)
             lora(3, t + 1)
             if r == 2 and g < NG:
                 o_out(g - 1, 0, TPG)
@@ -388,7 +427,9 @@ def tile_feedforward_pa_t_kernel(
                 o_out(NG - 1, 0, TPG - 1)
             if t == NT + 2:
                 o_out(NG - 1, TPG - 1, TPG)
-            if r == 0:
-                x_copy(g + 1, 1, nc.scalar.copy)
+            if xk == 1:
+                x_copy(xg_, 1, scopy)
             g_copy(t - 2)
+            if t == 1:
+                a2_copy()
             mx_pass(3, t + 2)

@@ -20,7 +20,6 @@ NT = TOKENS // P
 TPG = 4
 NG = NT // TPG
 WARM = 5
-GCUT = F
 FLOPS = 2 * TOKENS * (2 * D * F + 2 * R * F + F * R)
 
 
@@ -70,6 +69,7 @@ def tile_feedforward_pa_t_kernel(
 
         load_w(1, w1)
         nc.sync.dma_start(out=x_sb[0][:, 0 : 2 * D], in_=xv[:, 0 : 2 * D])
+        nc.sync.dma_start(out=x_sb[0][:, 2 * D : 4 * D], in_=xv[:, 2 * D : 4 * D])
         load_w(3, w3)
         load_xa(0)
         nc.sync.dma_start(
@@ -80,10 +80,9 @@ def tile_feedforward_pa_t_kernel(
             out=b_sb[:, 4 * R : 8 * R].rearrange("p (c r) -> p c r", c=4),
             in_=lora_B3.rearrange("(c p) r -> p c r", p=P),
         )
-        nc.sync.dma_start(out=x_sb[0][:, 2 * D : 4 * D], in_=xv[:, 2 * D : 4 * D])
         load_x(1)
-        load_xa(1)
         nc.sync.dma_start(out=a_sb[:], in_=lora_A2)
+        load_xa(1)
         for g in range(2, NG):
             load_x(g)
             load_xa(g)
@@ -167,37 +166,42 @@ def tile_feedforward_pa_t_kernel(
                 return
             copy(out=xaT[g][:], in_=abank[g][:])
 
-        def x_quant_part(h):
-            nc.vector.quantize_mx(
-                out=xc[0][:, 2 * P * h : 2 * P * (h + 1)].bitcast(FP8X4),
-                scales=xs[0][:, 2 * P * h : 2 * P * (h + 1)],
-                in_=xg[0][:, 8 * P * h : 8 * P * (h + 1)],
-            )
-
+        warm = keep.tile([P, F], BF16, name="warm")
+        nc.vector.memset(warm[:], 0.0)
+        wps = ps1.tile([P, F], F32, name="wps", tag="gt")
+        for i in range(WARM):
+            nc.tensor.matmul(out=wps[:], lhsT=warm[:, 0:P], rhs=warm[:], start=True, stop=True)
+        w_transposes(1, ("mx1", "mx3"))
+        x_transposes(0, 0)
+        x_transposes(0, 1)
+        w_transposes(3, ("l1", "l3"))
+        w_copy(1, 0, nc.scalar.copy)
+        w_copy(1, 1, nc.vector.tensor_copy)
+        x_copy(0, 0, nc.scalar.copy)
+        x_copy(0, 1, nc.vector.tensor_copy)
+        w_quant(1)
+        w_copy(3, 0, nc.scalar.copy)
+        w_copy(3, 1, nc.vector.tensor_copy)
+        x_quant(0)
+        xa_transposes(0)
+        xa_copy(0, nc.scalar.copy)
+        bbank = ps1.tile([P, 2 * F], BF16, name="bbank", tag="gt")
+        for i in range(8):
+            nc.tensor.transpose(bbank[:, P * i : P * (i + 1)], b_sb[:, R * i : R * (i + 1)], ident_b[:])
         bT = keep.tile([P, 2 * F], BF16, name="bT")
-        bbank = {}
-
-        def b_transposes():
-            bbank[0] = ps1.tile([P, 2 * F], BF16, name="bbank", tag="gt")
-            for i in range(8):
-                nc.tensor.transpose(
-                    bbank[0][:, P * i : P * (i + 1)], b_sb[:, R * i : R * (i + 1)], ident_b[:]
-                )
-
+        nc.scalar.copy(out=bT[:], in_=bbank[:])
+        w_quant(3)
+        a2bank = ps1.tile([P, 4, P], BF16, name="a2bank", tag="o")
+        for c in range(4):
+            nc.tensor.transpose(a2bank[:, c, :], a_sb[:, P * c : P * (c + 1)], ident_b[:])
         ag = keep.tile([P, 4 * R], BF16, name="ag", align_bytes=64)
         ac = keep.tile([P, R], U32, name="ac", align_bytes=64)
         asc = keep.tile([P, R], U8, name="asc", align_bytes=64)
-        a2bank = {}
-
-        def a2_transposes():
-            a2bank[0] = ps1.tile([P, 4, P], BF16, name="a2bank", tag="o")
-            for c in range(4):
-                nc.tensor.transpose(a2bank[0][:, c, :], a_sb[:, P * c : P * (c + 1)], ident_b[:])
 
         def a2_copy():
             nc.vector.tensor_copy(
                 out=ag[:].rearrange("p (r c) -> p r c", c=4),
-                in_=a2bank[0][:].rearrange("p c r -> p r c"),
+                in_=a2bank[:].rearrange("p c r -> p r c"),
             )
 
         def a2_quant():
@@ -279,7 +283,7 @@ def tile_feedforward_pa_t_kernel(
             g, j = divmod(t, TPG)
             if j == 0:
                 g_sb[g] = rot3.tile([P, TPG * F], F32, name="g_sb", tag="g_sb")
-            cut = F // 2 if t == NT - 1 else GCUT
+            cut = F // 4 if t == NT - 1 else F
             nc.gpsimd.tensor_tensor(
                 out=g_sb[g][:, F * j : F * j + cut],
                 in0=s_sb[t][:, 0:cut],
@@ -302,7 +306,7 @@ def tile_feedforward_pa_t_kernel(
             if not ok(t):
                 return
             g, j = divmod(t, TPG)
-            gbank[t] = ps1.tile([P, 4, P], F32, name="gbank", tag="gt")
+            gbank[t] = ps1.tile([P, 4, P], F32, name="gbank", tag="mx1" if t == NT - 1 else "gt")
             for c in range(4):
                 c0 = F * j + P * c
                 nc.tensor.transpose(gbank[t][:, c, :], g_sb[g][:, c0 : c0 + P], ident_f[:])
@@ -311,7 +315,8 @@ def tile_feedforward_pa_t_kernel(
             if not ok(t):
                 return
             gg[t] = rot3.tile([P, 4 * P], BF16, name="gg", tag="gg", align_bytes=64)
-            nc.vector.tensor_copy(
+            copy = nc.scalar.copy if t == NT - 2 else nc.vector.tensor_copy
+            copy(
                 out=gg[t][:].rearrange("p (r c) -> p r c", c=4),
                 in_=gbank[t][:].rearrange("p c r -> p r c"),
             )
@@ -346,90 +351,47 @@ def tile_feedforward_pa_t_kernel(
             nc.scalar.copy(out=o_sb[:], in_=obank[g][:, j0:j1, :].rearrange("p j r -> p (j r)"))
             nc.sync.dma_start(out=ov[:, R * (TPG * g + j0) : R * (TPG * g + j1)], in_=o_sb[:])
 
-        vcopy = nc.vector.tensor_copy
-        scopy = nc.scalar.copy
-
-        warm = keep.tile([P, F], BF16, name="warm")
-        nc.vector.memset(warm[:], 0.0)
-        wps = ps1.tile([P, F], F32, name="wps", tag="gt")
-        for i in range(WARM):
-            nc.tensor.matmul(out=wps[:], lhsT=warm[:, 0:P], rhs=warm[:], start=True, stop=True)
-
-        w_transposes(1, ("mx1", "mx3"))
-        w_copy(1, 0, scopy)
-        w_copy(1, 1, vcopy)
-        x_transposes(0, 0)
-        x_copy(0, 0, scopy)
-        w_quant(1)
-        w_transposes(3, ("l1", "l3"))
-        x_quant_part(0)
-        w_copy(3, 0, scopy)
-        w_copy(3, 1, vcopy)
-        xa_transposes(0)
-        b_transposes()
-        x_transposes(0, 1)
-        xa_copy(0, scopy)
-        w_quant(3)
-        vcopy(out=bT[:], in_=bbank[0][:])
-        x_copy(0, 1, vcopy)
-        x_quant_part(1)
-        mx_pass(1, 0)
-        mx_pass(3, 0)
-        mx_out(1, 0)
-        mx_out(3, 0)
-        lora(1, 0)
-        lora(3, 0)
-        mx_pass(1, 1)
-        mx_pass(3, 1)
-
-        step = {}
-        early = {}
-        for g in range(1, NG):
-            early[max(TPG * g - 7, 2 * g - 2)] = g
-            for k in range(3):
-                step[max(TPG * g - 5, 0) + k] = (g, k)
-
-        for t in range(NT + 3):
+        for t in range(-2, NT + 3):
             g, r = divmod(t, TPG)
-            xg_, xk = step.get(t, (NG, 3))
-            mx_out(1, t + 1)
-            g_transposes(t - 2)
             add(1, t)
-            x_transposes(early.get(t, NG), 0)
-            if xk == 0:
-                x_transposes(xg_, 1)
-            if xk == 1:
-                xa_transposes(xg_)
-            if t == 1:
-                a2_transposes()
-            lora(1, t + 1)
-            silu(t)
+            if r == 2 and t > 0:
+                xa_copy(g + 1, nc.scalar.copy)
+            mx_out(1, t + 1)
+            if r == 1 and t > 0:
+                xa_transposes(g + 1)
+            if r == 0:
+                x_transposes(g + 1, 1)
+            mx_out(3, t + 1)
             add(3, t)
             g_quant(t - 3)
-            mx_out(3, t + 1)
-            if xk == 0 and xg_ % 2 == 1:
-                x_copy(xg_, 0, scopy)
-            gate(t - 1)
-            if xk == 0 and xg_ % 2 == 0:
-                x_copy(xg_, 0, vcopy)
-            if xk == 2:
-                x_quant(xg_)
-            if t == 2:
+            if t == -1:
+                a2_copy()
+            if t == 0:
                 a2_quant()
+            if r == 1 and t > 0:
+                x_quant(g + 1)
+            gate(t - 1)
+            g_transposes(t - 2)
+            if r == 3 and t > 0:
+                x_transposes(g + 2, 0)
+            if t == 0:
+                x_transposes(1, 0)
+            g_copy(t - 2)
+            if t == 0:
+                x_copy(1, 0, nc.vector.tensor_copy)
+            silu(t)
+            if r == 0:
+                x_copy(g + 1, 1, nc.scalar.copy)
+            lora(1, t + 1)
             mx_pass(1, t + 2)
             ga2(t - 3)
-            if xk == 2:
-                xa_copy(xg_, scopy)
-            lora(3, t + 1)
             if r == 2 and g < NG:
                 o_out(g - 1, 0, TPG)
             if t == NT + 1:
                 o_out(NG - 1, 0, TPG - 1)
             if t == NT + 2:
                 o_out(NG - 1, TPG - 1, TPG)
-            if xk == 1:
-                x_copy(xg_, 1, scopy)
-            g_copy(t - 2)
-            if t == 1:
-                a2_copy()
             mx_pass(3, t + 2)
+            lora(3, t + 1)
+            if r == 3 and t > 0:
+                x_copy(g + 2, 0, nc.vector.tensor_copy)

@@ -20,6 +20,7 @@ NT = TOKENS // P
 TPG = 4
 NG = NT // TPG
 WARM = 5
+GCUT = F
 FLOPS = 2 * TOKENS * (2 * D * F + 2 * R * F + F * R)
 
 
@@ -69,7 +70,6 @@ def tile_feedforward_pa_t_kernel(
 
         load_w(1, w1)
         nc.sync.dma_start(out=x_sb[0][:, 0 : 2 * D], in_=xv[:, 0 : 2 * D])
-        nc.sync.dma_start(out=x_sb[0][:, 2 * D : 4 * D], in_=xv[:, 2 * D : 4 * D])
         load_w(3, w3)
         load_xa(0)
         nc.sync.dma_start(
@@ -80,9 +80,10 @@ def tile_feedforward_pa_t_kernel(
             out=b_sb[:, 4 * R : 8 * R].rearrange("p (c r) -> p c r", c=4),
             in_=lora_B3.rearrange("(c p) r -> p c r", p=P),
         )
+        nc.sync.dma_start(out=x_sb[0][:, 2 * D : 4 * D], in_=xv[:, 2 * D : 4 * D])
         load_x(1)
-        nc.sync.dma_start(out=a_sb[:], in_=lora_A2)
         load_xa(1)
+        nc.sync.dma_start(out=a_sb[:], in_=lora_A2)
         for g in range(2, NG):
             load_x(g)
             load_xa(g)
@@ -166,42 +167,37 @@ def tile_feedforward_pa_t_kernel(
                 return
             copy(out=xaT[g][:], in_=abank[g][:])
 
-        warm = keep.tile([P, F], BF16, name="warm")
-        nc.vector.memset(warm[:], 0.0)
-        wps = ps1.tile([P, F], F32, name="wps", tag="gt")
-        for i in range(WARM):
-            nc.tensor.matmul(out=wps[:], lhsT=warm[:, 0:P], rhs=warm[:], start=True, stop=True)
-        w_transposes(1, ("mx1", "mx3"))
-        x_transposes(0, 0)
-        x_transposes(0, 1)
-        w_transposes(3, ("l1", "l3"))
-        w_copy(1, 0, nc.scalar.copy)
-        w_copy(1, 1, nc.vector.tensor_copy)
-        x_copy(0, 0, nc.scalar.copy)
-        x_copy(0, 1, nc.vector.tensor_copy)
-        w_quant(1)
-        w_copy(3, 0, nc.scalar.copy)
-        w_copy(3, 1, nc.vector.tensor_copy)
-        x_quant(0)
-        xa_transposes(0)
-        xa_copy(0, nc.scalar.copy)
-        bbank = ps1.tile([P, 2 * F], BF16, name="bbank", tag="gt")
-        for i in range(8):
-            nc.tensor.transpose(bbank[:, P * i : P * (i + 1)], b_sb[:, R * i : R * (i + 1)], ident_b[:])
+        def x_quant_part(h):
+            nc.vector.quantize_mx(
+                out=xc[0][:, 2 * P * h : 2 * P * (h + 1)].bitcast(FP8X4),
+                scales=xs[0][:, 2 * P * h : 2 * P * (h + 1)],
+                in_=xg[0][:, 8 * P * h : 8 * P * (h + 1)],
+            )
+
         bT = keep.tile([P, 2 * F], BF16, name="bT")
-        nc.scalar.copy(out=bT[:], in_=bbank[:])
-        w_quant(3)
-        a2bank = ps1.tile([P, 4, P], BF16, name="a2bank", tag="o")
-        for c in range(4):
-            nc.tensor.transpose(a2bank[:, c, :], a_sb[:, P * c : P * (c + 1)], ident_b[:])
+        bbank = {}
+
+        def b_transposes():
+            bbank[0] = ps1.tile([P, 2 * F], BF16, name="bbank", tag="gt")
+            for i in range(8):
+                nc.tensor.transpose(
+                    bbank[0][:, P * i : P * (i + 1)], b_sb[:, R * i : R * (i + 1)], ident_b[:]
+                )
+
         ag = keep.tile([P, 4 * R], BF16, name="ag", align_bytes=64)
         ac = keep.tile([P, R], U32, name="ac", align_bytes=64)
         asc = keep.tile([P, R], U8, name="asc", align_bytes=64)
+        a2bank = {}
+
+        def a2_transposes():
+            a2bank[0] = ps1.tile([P, 4, P], BF16, name="a2bank", tag="o")
+            for c in range(4):
+                nc.tensor.transpose(a2bank[0][:, c, :], a_sb[:, P * c : P * (c + 1)], ident_b[:])
 
         def a2_copy():
             nc.vector.tensor_copy(
                 out=ag[:].rearrange("p (r c) -> p r c", c=4),
-                in_=a2bank[:].rearrange("p c r -> p r c"),
+                in_=a2bank[0][:].rearrange("p c r -> p r c"),
             )
 
         def a2_quant():
@@ -351,7 +347,43 @@ def tile_feedforward_pa_t_kernel(
             nc.scalar.copy(out=o_sb[:], in_=obank[g][:, j0:j1, :].rearrange("p j r -> p (j r)"))
             nc.sync.dma_start(out=ov[:, R * (TPG * g + j0) : R * (TPG * g + j1)], in_=o_sb[:])
 
-        for t in range(-2, NT + 3):
+        vcopy = nc.vector.tensor_copy
+        scopy = nc.scalar.copy
+
+        warm = keep.tile([P, F], BF16, name="warm")
+        nc.vector.memset(warm[:], 0.0)
+        wps = ps1.tile([P, F], F32, name="wps", tag="gt")
+        for i in range(WARM):
+            nc.tensor.matmul(out=wps[:], lhsT=warm[:, 0:P], rhs=warm[:], start=True, stop=True)
+
+        w_transposes(1, ("mx1", "mx3"))
+        w_copy(1, 0, scopy)
+        w_copy(1, 1, vcopy)
+        x_transposes(0, 0)
+        x_copy(0, 0, scopy)
+        w_quant(1)
+        w_transposes(3, ("l1", "l3"))
+        x_quant_part(0)
+        w_copy(3, 0, scopy)
+        w_copy(3, 1, vcopy)
+        xa_transposes(0)
+        b_transposes()
+        x_transposes(0, 1)
+        xa_copy(0, scopy)
+        w_quant(3)
+        vcopy(out=bT[:], in_=bbank[0][:])
+        x_copy(0, 1, vcopy)
+        x_quant_part(1)
+        mx_pass(1, 0)
+        mx_pass(3, 0)
+        mx_out(1, 0)
+        mx_out(3, 0)
+        lora(1, 0)
+        lora(3, 0)
+        mx_pass(1, 1)
+        mx_pass(3, 1)
+
+        for t in range(NT + 3):
             g, r = divmod(t, TPG)
             add(1, t)
             if r == 2 and t > 0:
@@ -359,14 +391,14 @@ def tile_feedforward_pa_t_kernel(
             mx_out(1, t + 1)
             if r == 1 and t > 0:
                 xa_transposes(g + 1)
+            if t == 1:
+                a2_transposes()
             if r == 0:
                 x_transposes(g + 1, 1)
             mx_out(3, t + 1)
             add(3, t)
             g_quant(t - 3)
-            if t == -1:
-                a2_copy()
-            if t == 0:
+            if t == 2:
                 a2_quant()
             if r == 1 and t > 0:
                 x_quant(g + 1)
@@ -379,6 +411,8 @@ def tile_feedforward_pa_t_kernel(
             g_copy(t - 2)
             if t == 0:
                 x_copy(1, 0, nc.vector.tensor_copy)
+            if t == 1:
+                a2_copy()
             silu(t)
             if r == 0:
                 x_copy(g + 1, 1, nc.scalar.copy)

@@ -17,10 +17,10 @@ D = 512
 F = 512
 R = 128
 NT = TOKENS // P
+NQ = NT // 2
 TPG = 4
 NG = NT // TPG
 WARM = 5
-GCUT = F
 FLOPS = 2 * TOKENS * (2 * D * F + 2 * R * F + F * R)
 
 
@@ -40,7 +40,6 @@ def tile_feedforward_pa_t_kernel(
         rot2 = ctx.enter_context(tc.tile_pool(name="rot2", bufs=2))
         rot3 = ctx.enter_context(tc.tile_pool(name="rot3", bufs=3))
         ps1 = ctx.enter_context(tc.psum_pool(name="ps1", bufs=1))
-        ps2 = ctx.enter_context(tc.psum_pool(name="ps2", bufs=2))
 
         w_sb = {}
         for k in (1, 3):
@@ -93,6 +92,9 @@ def tile_feedforward_pa_t_kernel(
         ident_b = keep.tile([P, P], BF16, name="ident_b")
         make_identity(nc, ident_b[:])
 
+        vcopy = nc.vector.tensor_copy
+        scopy = nc.scalar.copy
+
         def word_transposes(words, bank):
             for a in range(2):
                 for u in range(2):
@@ -113,16 +115,6 @@ def tile_feedforward_pa_t_kernel(
             wg[k] = keep.tile([P, 4 * F], BF16, name="wg%d" % k, align_bytes=64)
             wc[k] = keep.tile([P, F], U32, name="wc%d" % k, align_bytes=64)
             ws[k] = keep.tile([P, F], U8, name="ws%d" % k, align_bytes=64)
-        xg = {}
-        xc = {}
-        xs = {}
-        xaT = {}
-        xbank = {}
-        abank = {}
-        for g in range(NG):
-            xc[g] = keep.tile([P, TPG * P], U32, name="xc%d" % g, align_bytes=64)
-            xs[g] = keep.tile([P, TPG * P], U8, name="xs%d" % g, align_bytes=64)
-            xaT[g] = keep.tile([P, 2 * TPG * P], BF16, name="xaT%d" % g)
 
         def w_transposes(k, tags):
             for h in range(2):
@@ -135,44 +127,52 @@ def tile_feedforward_pa_t_kernel(
         def w_quant(k):
             nc.vector.quantize_mx(out=wc[k][:].bitcast(FP8X4), scales=ws[k][:], in_=wg[k][:])
 
-        def x_transposes(g, h):
-            if not 0 <= g < NG:
-                return
-            xbank[(g, h)] = ps2.tile([P, 2, 2, P], F32, name="xbank", tag="misc")
-            word_transposes(x_sb[g][:].bitcast(F32)[:, 512 * h : 512 * h + 512], xbank[(g, h)])
+        xg = {}
+        xc = {}
+        xs = {}
+        xaT = {}
+        xbank = {}
+        abank = {}
+        for q in range(NQ):
+            xc[q] = keep.tile([P, 2 * P], U32, name="xc%d" % q, align_bytes=64)
+            xs[q] = keep.tile([P, 2 * P], U8, name="xs%d" % q, align_bytes=64)
 
-        def x_copy(g, h, copy):
-            if not 0 <= g < NG:
+        def x_transposes(q, tag="x"):
+            if not 0 <= q < NQ:
                 return
-            if h == 0:
-                xg[g] = rot2.tile([P, 4 * TPG * P], BF16, name="xg", tag="xg", align_bytes=64)
-            word_copy(copy, xg[g][:].bitcast(F32)[:, 512 * h : 512 * h + 512], xbank[(g, h)])
+            g, h = divmod(q, 2)
+            xbank[q] = ps1.tile([P, 2, 2, P], F32, name="xbank", tag=tag)
+            word_transposes(x_sb[g][:].bitcast(F32)[:, 512 * h : 512 * h + 512], xbank[q])
 
-        def x_quant(g):
-            if not 0 <= g < NG:
+        def x_copy(q, copy):
+            if not 0 <= q < NQ:
                 return
-            nc.vector.quantize_mx(out=xc[g][:].bitcast(FP8X4), scales=xs[g][:], in_=xg[g][:])
+            xg[q] = rot3.tile([P, 8 * P], BF16, name="xg", tag="xg", align_bytes=64)
+            word_copy(copy, xg[q][:].bitcast(F32), xbank[q])
 
-        def xa_transposes(g):
-            if not 0 <= g < NG:
+        def x_quant(q):
+            if not 0 <= q < NQ:
                 return
-            abank[g] = ps2.tile([P, 2 * TPG * P], BF16, name="abank", tag="misc")
-            for i in range(2 * TPG):
-                nc.tensor.transpose(
-                    abank[g][:, P * i : P * (i + 1)], xa_sb[g][:, R * i : R * (i + 1)], ident_b[:]
-                )
+            nc.vector.quantize_mx(out=xc[q][:].bitcast(FP8X4), scales=xs[q][:], in_=xg[q][:])
 
-        def xa_copy(g, copy):
-            if not 0 <= g < NG:
+        def xa_transposes(q):
+            if not 0 <= q < NQ:
                 return
-            copy(out=xaT[g][:], in_=abank[g][:])
+            g, h = divmod(q, 2)
+            abank[q] = ps1.tile([P, 8 * P], BF16, name="abank", tag="xa")
+            for b in range(2):
+                for j in range(2):
+                    i = TPG * b + 2 * h + j
+                    n = 2 * b + j
+                    nc.tensor.transpose(
+                        abank[q][:, P * n : P * (n + 1)], xa_sb[g][:, R * i : R * (i + 1)], ident_b[:]
+                    )
 
-        def x_quant_part(h):
-            nc.vector.quantize_mx(
-                out=xc[0][:, 2 * P * h : 2 * P * (h + 1)].bitcast(FP8X4),
-                scales=xs[0][:, 2 * P * h : 2 * P * (h + 1)],
-                in_=xg[0][:, 8 * P * h : 8 * P * (h + 1)],
-            )
+        def xa_copy(q, copy):
+            if not 0 <= q < NQ:
+                return
+            xaT[q] = rot3.tile([P, 4 * P], BF16, name="xaT", tag="xaT")
+            copy(out=xaT[q][:], in_=abank[q][:, 0 : 4 * P])
 
         bT = keep.tile([P, 2 * F], BF16, name="bT")
         bbank = {}
@@ -190,14 +190,16 @@ def tile_feedforward_pa_t_kernel(
         a2bank = {}
 
         def a2_transposes():
-            a2bank[0] = ps1.tile([P, 4, P], BF16, name="a2bank", tag="o")
-            for c in range(4):
-                nc.tensor.transpose(a2bank[0][:, c, :], a_sb[:, P * c : P * (c + 1)], ident_b[:])
+            a2bank[0] = ps1.tile([P, 4, P], F32, name="a2bank", tag="o")
+            for u in range(2):
+                nc.tensor.transpose(
+                    a2bank[0][:, u, :], a_sb[:].bitcast(F32)[:, P * u : P * (u + 1)], ident_f[:]
+                )
 
         def a2_copy():
-            nc.vector.tensor_copy(
-                out=ag[:].rearrange("p (r c) -> p r c", c=4),
-                in_=a2bank[0][:].rearrange("p c r -> p r c"),
+            vcopy(
+                out=ag[:].bitcast(F32).rearrange("p (r u) -> p r u", u=2),
+                in_=a2bank[0][:, 0:2, :].rearrange("p u r -> p r u"),
             )
 
         def a2_quant():
@@ -209,6 +211,7 @@ def tile_feedforward_pa_t_kernel(
         h_sb = {}
         s_sb = {}
         g_sb = {}
+        gb_sb = {}
         gbank = {}
         gg = {}
         gc = {}
@@ -221,12 +224,12 @@ def tile_feedforward_pa_t_kernel(
         def mx_pass(k, t):
             if not ok(t):
                 return
-            g, j = divmod(t, TPG)
+            q, j = divmod(t, 2)
             mx[(k, t)] = ps1.tile([P, F], F32, name="mx%d" % k, tag="mx%d" % k)
             nc.tensor.matmul_mx(
                 out=mx[(k, t)][:],
-                lhsT=xc[g][:, P * j : P * (j + 1)].bitcast(FP8X4),
-                lhsT_scale=xs[g][:, P * j : P * (j + 1)],
+                lhsT=xc[q][:, P * j : P * (j + 1)].bitcast(FP8X4),
+                lhsT_scale=xs[q][:, P * j : P * (j + 1)],
                 rhs=wc[k][:].bitcast(FP8X4),
                 rhs_scale=ws[k][:],
                 start=True,
@@ -236,14 +239,14 @@ def tile_feedforward_pa_t_kernel(
         def lora(k, t):
             if not ok(t):
                 return
-            g, j = divmod(t, TPG)
-            half = 0 if k == 1 else 1
-            i = TPG * half + j
+            q, j = divmod(t, 2)
+            b = 0 if k == 1 else 1
+            n = 2 * b + j
             lo[(k, t)] = ps1.tile([P, F], F32, name="l%d" % k, tag="l%d" % k)
             nc.tensor.matmul(
                 out=lo[(k, t)][:],
-                lhsT=xaT[g][:, P * i : P * (i + 1)],
-                rhs=bT[:, F * half : F * (half + 1)],
+                lhsT=xaT[q][:, P * n : P * (n + 1)],
+                rhs=bT[:, F * b : F * (b + 1)],
                 start=True,
                 stop=True,
             )
@@ -252,7 +255,7 @@ def tile_feedforward_pa_t_kernel(
             if not ok(t):
                 return
             m_sb[(k, t)] = rot3.tile([P, F], F32, name="m%d" % k, tag="m%d" % k)
-            nc.scalar.copy(out=m_sb[(k, t)][:], in_=mx[(k, t)][:])
+            scopy(out=m_sb[(k, t)][:], in_=mx[(k, t)][:])
 
         def add(k, t):
             if not ok(t):
@@ -273,82 +276,115 @@ def tile_feedforward_pa_t_kernel(
             s_sb[t] = rot3.tile([P, F], F32, name="s1", tag="s1")
             nc.scalar.activation(out=s_sb[t][:], in_=h_sb[(1, t)][:], func=ACT.Silu)
 
+        def product(engine, t, c0, c1):
+            j = t % 2
+            engine.tensor_tensor(
+                out=g_sb[t // 2][:, F * j + c0 : F * j + c1],
+                in0=s_sb[t][:, c0:c1],
+                in1=h_sb[(3, t)][:, c0:c1],
+                op=ALU.mult,
+            )
+
+        def store_g(q):
+            nc.sync.dma_start(out=gv[:, 2 * F * q : 2 * F * (q + 1)], in_=g_sb[q][:])
+
         def gate(t):
             if not ok(t):
                 return
-            g, j = divmod(t, TPG)
+            q, j = divmod(t, 2)
             if j == 0:
-                g_sb[g] = rot3.tile([P, TPG * F], F32, name="g_sb", tag="g_sb")
-            cut = F // 4 if t == NT - 1 else F
-            nc.gpsimd.tensor_tensor(
-                out=g_sb[g][:, F * j : F * j + cut],
-                in0=s_sb[t][:, 0:cut],
-                in1=h_sb[(3, t)][:, 0:cut],
-                op=ALU.mult,
-            )
-            if cut < F:
-                nc.vector.tensor_tensor(
-                    out=g_sb[g][:, F * j + cut : F * (j + 1)],
-                    in0=s_sb[t][:, cut:F],
-                    in1=h_sb[(3, t)][:, cut:F],
-                    op=ALU.mult,
+                g_sb[q] = rot3.tile([P, 2 * F], F32, name="g_sb", tag="g_sb")
+                gb_sb[q] = rot3.tile([P, 2 * F], BF16, name="gb_sb", tag="gb_sb")
+            if t == NT - 1:
+                product(nc.gpsimd, t, 0, F // 4)
+                product(nc.vector, t, F // 4, F)
+            else:
+                product(nc.gpsimd, t, 0, F)
+            if t < NT - 2:
+                nc.gpsimd.tensor_scalar(
+                    out=gb_sb[q][:, F * j : F * (j + 1)],
+                    in0=g_sb[q][:, F * j : F * (j + 1)],
+                    scalar1=1.0,
+                    scalar2=0.0,
+                    op0=ALU.mult,
+                    op1=ALU.add,
                 )
-            if j % 2 == 1:
-                nc.sync.dma_start(
-                    out=gv[:, F * (t - 1) : F * (t + 1)], in_=g_sb[g][:, F * (j - 1) : F * (j + 1)]
-                )
+            if j == 1:
+                store_g(q)
 
-        def g_transposes(t):
-            if not ok(t):
+        def g_transposes(q):
+            if not 0 <= q < NQ - 1:
                 return
-            g, j = divmod(t, TPG)
-            gbank[t] = ps1.tile([P, 4, P], F32, name="gbank", tag="mx1" if t == NT - 1 else "gt")
-            for c in range(4):
-                c0 = F * j + P * c
-                nc.tensor.transpose(gbank[t][:, c, :], g_sb[g][:, c0 : c0 + P], ident_f[:])
+            gbank[q] = ps1.tile([P, 2, 2, P], F32, name="gbank", tag="gt")
+            word_transposes(gb_sb[q][:].bitcast(F32), gbank[q])
 
-        def g_copy(t):
-            if not ok(t):
+        def g_copy(q, copy):
+            if not 0 <= q < NQ - 1:
                 return
-            gg[t] = rot3.tile([P, 4 * P], BF16, name="gg", tag="gg", align_bytes=64)
-            copy = nc.scalar.copy if t == NT - 2 else nc.vector.tensor_copy
-            copy(
-                out=gg[t][:].rearrange("p (r c) -> p r c", c=4),
-                in_=gbank[t][:].rearrange("p c r -> p r c"),
-            )
+            gg[q] = rot2.tile([P, 8 * P], BF16, name="gg", tag="gg", align_bytes=64)
+            word_copy(copy, gg[q][:].bitcast(F32), gbank[q])
 
-        def g_quant(t):
-            if not ok(t):
+        def g_quant(q):
+            if not 0 <= q < NQ - 1:
                 return
-            gc[t] = rot3.tile([P, P], U32, name="gc", tag="gc", align_bytes=64)
-            gs[t] = rot3.tile([P, P], U8, name="gs", tag="gs", align_bytes=64)
-            nc.vector.quantize_mx(out=gc[t][:].bitcast(FP8X4), scales=gs[t][:], in_=gg[t][:])
+            gc[q] = rot2.tile([P, 2 * P], U32, name="gc", tag="gc", align_bytes=64)
+            gs[q] = rot2.tile([P, 2 * P], U8, name="gs", tag="gs", align_bytes=64)
+            nc.vector.quantize_mx(out=gc[q][:].bitcast(FP8X4), scales=gs[q][:], in_=gg[q][:])
 
-        def ga2(t):
-            if not ok(t):
-                return
-            g, j = divmod(t, TPG)
-            if j == 0:
-                obank[g] = ps1.tile([P, TPG, R], F32, name="obank", tag="o")
+        def ga2_pass(out, codes, scales):
             nc.tensor.matmul_mx(
-                out=obank[g][:, j, :],
-                lhsT=gc[t][:].bitcast(FP8X4),
-                lhsT_scale=gs[t][:],
+                out=out,
+                lhsT=codes.bitcast(FP8X4),
+                lhsT_scale=scales,
                 rhs=ac[:].bitcast(FP8X4),
                 rhs_scale=asc[:],
                 start=True,
                 stop=True,
             )
 
-        def o_out(g, j0, j1):
-            if not 0 <= g < NG:
+        def ga2(q):
+            if not 0 <= q < NQ - 1:
                 return
-            o_sb = rot2.tile([P, (j1 - j0) * R], F32, name="o_sb", tag="o_sb%d" % (j1 - j0))
-            nc.scalar.copy(out=o_sb[:], in_=obank[g][:, j0:j1, :].rearrange("p j r -> p (j r)"))
-            nc.sync.dma_start(out=ov[:, R * (TPG * g + j0) : R * (TPG * g + j1)], in_=o_sb[:])
+            obank[q] = ps1.tile([P, 4, R], F32, name="obank", tag="o")
+            for j in range(2):
+                cols = slice(P * j, P * (j + 1))
+                ga2_pass(obank[q][:, j, :], gc[q][:, cols], gs[q][:, cols])
 
-        vcopy = nc.vector.tensor_copy
-        scopy = nc.scalar.copy
+        def o_out(q):
+            if not 0 <= q < NQ - 1:
+                return
+            o_sb = rot2.tile([P, 2 * R], F32, name="o_sb", tag="o_sb")
+            scopy(out=o_sb[:], in_=obank[q][:, 0:2, :].rearrange("p j r -> p (j r)"))
+            nc.sync.dma_start(out=ov[:, 2 * R * q : 2 * R * (q + 1)], in_=o_sb[:])
+
+        def last_transposes(t, tag):
+            q, j = divmod(t, 2)
+            gbank[t] = ps1.tile([P, 4, P], F32, name="lbank", tag=tag)
+            for c in range(4):
+                u, e = divmod(c, 2)
+                c0 = F * j + 256 * u + e
+                nc.tensor.transpose(
+                    gbank[t][:, c, :], g_sb[q][:, c0 : F * j + 256 * (u + 1) : 2], ident_f[:]
+                )
+
+        def last_copy(t, copy):
+            gg[t] = keep.tile([P, 4 * P], BF16, name="lgg%d" % t, align_bytes=64)
+            copy(
+                out=gg[t][:].rearrange("p (r c) -> p r c", c=4),
+                in_=gbank[t][:].rearrange("p c r -> p r c"),
+            )
+
+        def last_quant(t):
+            gc[t] = keep.tile([P, P], U32, name="lgc%d" % t, align_bytes=64)
+            gs[t] = keep.tile([P, P], U8, name="lgs%d" % t, align_bytes=64)
+            nc.vector.quantize_mx(out=gc[t][:].bitcast(FP8X4), scales=gs[t][:], in_=gg[t][:])
+
+        def last_out(t, tag):
+            ob = ps1.tile([P, 4, R], F32, name="lob", tag=tag)
+            ga2_pass(ob[:, 0, :], gc[t][:], gs[t][:])
+            o_sb = keep.tile([P, R], F32, name="lo_sb%d" % t)
+            scopy(out=o_sb[:], in_=ob[:, 0, :])
+            nc.sync.dma_start(out=ov[:, R * t : R * (t + 1)], in_=o_sb[:])
 
         warm = keep.tile([P, F], BF16, name="warm")
         nc.vector.memset(warm[:], 0.0)
@@ -356,76 +392,78 @@ def tile_feedforward_pa_t_kernel(
         for i in range(WARM):
             nc.tensor.matmul(out=wps[:], lhsT=warm[:, 0:P], rhs=warm[:], start=True, stop=True)
 
+        dummy = keep.tile([P, 1], F32, name="dummy")
+        nc.scalar.activation(out=dummy[:], in_=ident_f[:, 0:1], func=ACT.Silu)
+
         w_transposes(1, ("mx1", "mx3"))
         w_copy(1, 0, scopy)
         w_copy(1, 1, vcopy)
-        x_transposes(0, 0)
-        x_copy(0, 0, scopy)
+        x_transposes(0)
+        x_copy(0, scopy)
         w_quant(1)
         w_transposes(3, ("l1", "l3"))
-        x_quant_part(0)
+        x_quant(0)
         w_copy(3, 0, scopy)
         w_copy(3, 1, vcopy)
         xa_transposes(0)
         b_transposes()
-        x_transposes(0, 1)
+        x_transposes(1)
         xa_copy(0, scopy)
         w_quant(3)
         vcopy(out=bT[:], in_=bbank[0][:])
-        x_copy(0, 1, vcopy)
-        x_quant_part(1)
         mx_pass(1, 0)
         mx_pass(3, 0)
+        x_copy(1, scopy)
         mx_out(1, 0)
+        x_quant(1)
         mx_out(3, 0)
         lora(1, 0)
         lora(3, 0)
         mx_pass(1, 1)
         mx_pass(3, 1)
+        x_transposes(2)
+        xa_transposes(1)
 
-        for t in range(NT + 3):
-            g, r = divmod(t, TPG)
+        for t in range(NT):
+            q, r = divmod(t, 2)
+            if r == 1:
+                x_transposes(q + 3)
+                xa_transposes(q + 2)
+                g_transposes(q - 1)
             add(1, t)
-            if r == 2 and t > 0:
-                xa_copy(g + 1, nc.scalar.copy)
             mx_out(1, t + 1)
-            if r == 1 and t > 0:
-                xa_transposes(g + 1)
-            if t == 1:
-                a2_transposes()
-            if r == 0:
-                x_transposes(g + 1, 1)
-            mx_out(3, t + 1)
-            add(3, t)
-            g_quant(t - 3)
-            if t == 2:
-                a2_quant()
-            if r == 1 and t > 0:
-                x_quant(g + 1)
-            gate(t - 1)
-            g_transposes(t - 2)
-            if r == 3 and t > 0:
-                x_transposes(g + 2, 0)
-            if t == 0:
-                x_transposes(1, 0)
-            g_copy(t - 2)
-            if t == 0:
-                x_copy(1, 0, nc.vector.tensor_copy)
-            if t == 1:
-                a2_copy()
-            silu(t)
-            if r == 0:
-                x_copy(g + 1, 1, nc.scalar.copy)
             lora(1, t + 1)
             mx_pass(1, t + 2)
-            ga2(t - 3)
-            if r == 2 and g < NG:
-                o_out(g - 1, 0, TPG)
-            if t == NT + 1:
-                o_out(NG - 1, 0, TPG - 1)
-            if t == NT + 2:
-                o_out(NG - 1, TPG - 1, TPG)
-            mx_pass(3, t + 2)
+            add(3, t)
+            silu(t)
+            mx_out(3, t + 1)
             lora(3, t + 1)
-            if r == 3 and t > 0:
-                x_copy(g + 2, 0, nc.vector.tensor_copy)
+            if t == 2:
+                a2_transposes()
+                a2_copy()
+            if t == 3:
+                a2_quant()
+            if r == 0:
+                g_quant(q - 2)
+                x_copy(q + 2, vcopy)
+                xa_copy(q + 1, scopy)
+                ga2(q - 2)
+            else:
+                g_copy(q - 1, vcopy)
+                x_quant(q + 2)
+                o_out(q - 2)
+            mx_pass(3, t + 2)
+            gate(t)
+            if t == NT - 1:
+                last_transposes(NT - 2, "x")
+
+        last_copy(NT - 2, scopy)
+        g_quant(NQ - 2)
+        last_transposes(NT - 1, "xa")
+        last_quant(NT - 2)
+        ga2(NQ - 2)
+        o_out(NQ - 2)
+        last_copy(NT - 1, vcopy)
+        last_quant(NT - 1)
+        last_out(NT - 2, "x")
+        last_out(NT - 1, "xa")

@@ -38,8 +38,11 @@ def tile_feedforward_pa_t_kernel(
         ctx.enter_context(tc.manual_schedule())
         keep = ctx.enter_context(tc.tile_pool(name="keep", bufs=1))
         rot2 = ctx.enter_context(tc.tile_pool(name="rot2", bufs=2))
+        rot4 = ctx.enter_context(tc.tile_pool(name="rot4", bufs=4))
         rot3 = ctx.enter_context(tc.tile_pool(name="rot3", bufs=3))
         ps1 = ctx.enter_context(tc.psum_pool(name="ps1", bufs=1))
+        psm = ctx.enter_context(tc.psum_pool(name="psm", bufs=2))
+        psl = ctx.enter_context(tc.psum_pool(name="psl", bufs=3))
 
         w_sb = {}
         for k in (1, 3):
@@ -80,7 +83,11 @@ def tile_feedforward_pa_t_kernel(
             in_=lora_B3.rearrange("(c p) r -> p c r", p=P),
         )
         nc.sync.dma_start(out=x_sb[0][:, 2 * D : 4 * D], in_=xv[:, 2 * D : 4 * D])
-        load_x(1)
+        for h in range(2):
+            nc.sync.dma_start(
+                out=x_sb[1][:, 2 * D * h : 2 * D * (h + 1)],
+                in_=xv[:, 2 * D * (h + 2) : 2 * D * (h + 3)],
+            )
         load_xa(1)
         nc.sync.dma_start(out=a_sb[:], in_=lora_A2)
         for g in range(2, NG):
@@ -116,9 +123,9 @@ def tile_feedforward_pa_t_kernel(
             wc[k] = keep.tile([P, F], U32, name="wc%d" % k, align_bytes=64)
             ws[k] = keep.tile([P, F], U8, name="ws%d" % k, align_bytes=64)
 
-        def w_transposes(k, tags):
+        def w_transposes(k, pool, tag):
             for h in range(2):
-                wbank[(k, h)] = ps1.tile([P, 2, 2, P], F32, name="wbank", tag=tags[h])
+                wbank[(k, h)] = pool.tile([P, 2, 2, P], F32, name="wbank", tag=tag)
                 word_transposes(w_sb[k][:].bitcast(F32)[:, 512 * h : 512 * h + 512], wbank[(k, h)])
 
         def w_copy(k, h, copy):
@@ -127,15 +134,33 @@ def tile_feedforward_pa_t_kernel(
         def w_quant(k):
             nc.vector.quantize_mx(out=wc[k][:].bitcast(FP8X4), scales=ws[k][:], in_=wg[k][:])
 
-        xg = {}
+        gc = {}
+        gs = {}
         xc = {}
         xs = {}
         xaT = {}
         xbank = {}
         abank = {}
-        for q in range(NQ):
-            xc[q] = keep.tile([P, 2 * P], U32, name="xc%d" % q, align_bytes=64)
-            xs[q] = keep.tile([P, 2 * P], U8, name="xs%d" % q, align_bytes=64)
+        zg = {}
+
+        def z_half(q, part):
+            if q not in zg:
+                zg[q] = rot3.tile([P, 16 * P], BF16, name="zg", tag="zg", align_bytes=64)
+            return zg[q][:, 8 * P * part : 8 * P * (part + 1)]
+
+        def z_quant(q):
+            lo, hi = (1 if q < 3 else 0), (1 if q + 2 >= NQ else 2)
+            if hi <= lo:
+                return
+            zc = rot4.tile([P, 4 * P], U32, name="zc", tag="zc", align_bytes=64)
+            zs = rot4.tile([P, 4 * P], U8, name="zs", tag="zs", align_bytes=64)
+            nc.vector.quantize_mx(
+                out=zc[:, 2 * P * lo : 2 * P * hi].bitcast(FP8X4),
+                scales=zs[:, 2 * P * lo : 2 * P * hi],
+                in_=zg[q][:, 8 * P * lo : 8 * P * hi],
+            )
+            gc[q - 3], gs[q - 3] = zc[:, 0 : 2 * P], zs[:, 0 : 2 * P]
+            xc[q + 2], xs[q + 2] = zc[:, 2 * P : 4 * P], zs[:, 2 * P : 4 * P]
 
         def x_transposes(q, tag="x"):
             if not 0 <= q < NQ:
@@ -147,19 +172,13 @@ def tile_feedforward_pa_t_kernel(
         def x_copy(q, copy):
             if not 0 <= q < NQ:
                 return
-            xg[q] = rot3.tile([P, 8 * P], BF16, name="xg", tag="xg", align_bytes=64)
-            word_copy(copy, xg[q][:].bitcast(F32), xbank[q])
-
-        def x_quant(q):
-            if not 0 <= q < NQ:
-                return
-            nc.vector.quantize_mx(out=xc[q][:].bitcast(FP8X4), scales=xs[q][:], in_=xg[q][:])
+            word_copy(copy, z_half(q - 2, 1).bitcast(F32), xbank[q])
 
         def xa_transposes(q):
             if not 0 <= q < NQ:
                 return
             g, h = divmod(q, 2)
-            abank[q] = ps1.tile([P, 8 * P], BF16, name="abank", tag="xa")
+            abank[q] = ps1.tile([P, 8 * P], BF16, name="abank", tag="xo")
             for b in range(2):
                 for j in range(2):
                     i = TPG * b + 2 * h + j
@@ -190,7 +209,7 @@ def tile_feedforward_pa_t_kernel(
         a2bank = {}
 
         def a2_transposes():
-            a2bank[0] = ps1.tile([P, 4, P], F32, name="a2bank", tag="o")
+            a2bank[0] = ps1.tile([P, 4, P], F32, name="a2bank", tag="gt")
             for u in range(2):
                 nc.tensor.transpose(
                     a2bank[0][:, u, :], a_sb[:].bitcast(F32)[:, P * u : P * (u + 1)], ident_f[:]
@@ -214,8 +233,6 @@ def tile_feedforward_pa_t_kernel(
         gb_sb = {}
         gbank = {}
         gg = {}
-        gc = {}
-        gs = {}
         obank = {}
 
         def ok(t):
@@ -225,7 +242,7 @@ def tile_feedforward_pa_t_kernel(
             if not ok(t):
                 return
             q, j = divmod(t, 2)
-            mx[(k, t)] = ps1.tile([P, F], F32, name="mx%d" % k, tag="mx%d" % k)
+            mx[(k, t)] = psm.tile([P, F], F32, name="mx", tag="mx")
             nc.tensor.matmul_mx(
                 out=mx[(k, t)][:],
                 lhsT=xc[q][:, P * j : P * (j + 1)].bitcast(FP8X4),
@@ -242,7 +259,7 @@ def tile_feedforward_pa_t_kernel(
             q, j = divmod(t, 2)
             b = 0 if k == 1 else 1
             n = 2 * b + j
-            lo[(k, t)] = ps1.tile([P, F], F32, name="l%d" % k, tag="l%d" % k)
+            lo[(k, t)] = psl.tile([P, F], F32, name="lo", tag="l")
             nc.tensor.matmul(
                 out=lo[(k, t)][:],
                 lhsT=xaT[q][:, P * n : P * (n + 1)],
@@ -294,23 +311,29 @@ def tile_feedforward_pa_t_kernel(
             q, j = divmod(t, 2)
             if j == 0:
                 g_sb[q] = rot3.tile([P, 2 * F], F32, name="g_sb", tag="g_sb")
-                gb_sb[q] = rot3.tile([P, 2 * F], BF16, name="gb_sb", tag="gb_sb")
             if t == NT - 1:
                 product(nc.gpsimd, t, 0, F // 4)
                 product(nc.vector, t, F // 4, F)
             else:
                 product(nc.gpsimd, t, 0, F)
-            if t < NT - 2:
-                nc.gpsimd.tensor_scalar(
-                    out=gb_sb[q][:, F * j : F * (j + 1)],
-                    in0=g_sb[q][:, F * j : F * (j + 1)],
-                    scalar1=1.0,
-                    scalar2=0.0,
-                    op0=ALU.mult,
-                    op1=ALU.add,
-                )
             if j == 1:
                 store_g(q)
+
+        def g_cast(q):
+            if not 0 <= q < NQ - 1:
+                return
+            gb_sb[q] = rot2.tile([P, 2 * F], BF16, name="gb_sb", tag="gb_sb")
+            if q == NQ - 2:
+                scopy(out=gb_sb[q][:], in_=g_sb[q][:])
+                return
+            nc.gpsimd.tensor_scalar(
+                out=gb_sb[q][:],
+                in0=g_sb[q][:],
+                scalar1=1.0,
+                scalar2=0.0,
+                op0=ALU.mult,
+                op1=ALU.add,
+            )
 
         def g_transposes(q):
             if not 0 <= q < NQ - 1:
@@ -321,15 +344,7 @@ def tile_feedforward_pa_t_kernel(
         def g_copy(q, copy):
             if not 0 <= q < NQ - 1:
                 return
-            gg[q] = rot2.tile([P, 8 * P], BF16, name="gg", tag="gg", align_bytes=64)
-            word_copy(copy, gg[q][:].bitcast(F32), gbank[q])
-
-        def g_quant(q):
-            if not 0 <= q < NQ - 1:
-                return
-            gc[q] = rot2.tile([P, 2 * P], U32, name="gc", tag="gc", align_bytes=64)
-            gs[q] = rot2.tile([P, 2 * P], U8, name="gs", tag="gs", align_bytes=64)
-            nc.vector.quantize_mx(out=gc[q][:].bitcast(FP8X4), scales=gs[q][:], in_=gg[q][:])
+            word_copy(copy, z_half(q + 3, 0).bitcast(F32), gbank[q])
 
         def ga2_pass(out, codes, scales):
             nc.tensor.matmul_mx(
@@ -345,7 +360,10 @@ def tile_feedforward_pa_t_kernel(
         def ga2(q):
             if not 0 <= q < NQ - 1:
                 return
-            obank[q] = ps1.tile([P, 4, R], F32, name="obank", tag="o")
+            if q < NQ - 3:
+                obank[q] = ps1.tile([P, 4, R], F32, name="obank", tag="xo")
+            else:
+                obank[q] = psl.tile([P, 4, R], F32, name="obank", tag="l")
             for j in range(2):
                 cols = slice(P * j, P * (j + 1))
                 ga2_pass(obank[q][:, j, :], gc[q][:, cols], gs[q][:, cols])
@@ -354,12 +372,12 @@ def tile_feedforward_pa_t_kernel(
             if not 0 <= q < NQ - 1:
                 return
             o_sb = rot2.tile([P, 2 * R], F32, name="o_sb", tag="o_sb")
-            scopy(out=o_sb[:], in_=obank[q][:, 0:2, :].rearrange("p j r -> p (j r)"))
+            vcopy(out=o_sb[:], in_=obank[q][:, 0:2, :].rearrange("p j r -> p (j r)"))
             nc.sync.dma_start(out=ov[:, 2 * R * q : 2 * R * (q + 1)], in_=o_sb[:])
 
-        def last_transposes(t, tag):
+        def last_transposes(t):
             q, j = divmod(t, 2)
-            gbank[t] = ps1.tile([P, 4, P], F32, name="lbank", tag=tag)
+            gbank[t] = psm.tile([P, 4, P], F32, name="lbank", tag="mx")
             for c in range(4):
                 u, e = divmod(c, 2)
                 c0 = F * j + 256 * u + e
@@ -379,11 +397,11 @@ def tile_feedforward_pa_t_kernel(
             gs[t] = keep.tile([P, P], U8, name="lgs%d" % t, align_bytes=64)
             nc.vector.quantize_mx(out=gc[t][:].bitcast(FP8X4), scales=gs[t][:], in_=gg[t][:])
 
-        def last_out(t, tag):
-            ob = ps1.tile([P, 4, R], F32, name="lob", tag=tag)
+        def last_out(t, copy):
+            ob = psm.tile([P, 4, R], F32, name="lob", tag="mx")
             ga2_pass(ob[:, 0, :], gc[t][:], gs[t][:])
             o_sb = keep.tile([P, R], F32, name="lo_sb%d" % t)
-            scopy(out=o_sb[:], in_=ob[:, 0, :])
+            copy(out=o_sb[:], in_=ob[:, 0, :])
             nc.sync.dma_start(out=ov[:, R * t : R * (t + 1)], in_=o_sb[:])
 
         warm = keep.tile([P, F], BF16, name="warm")
@@ -395,75 +413,101 @@ def tile_feedforward_pa_t_kernel(
         dummy = keep.tile([P, 1], F32, name="dummy")
         nc.scalar.activation(out=dummy[:], in_=ident_f[:, 0:1], func=ACT.Silu)
 
-        w_transposes(1, ("mx1", "mx3"))
+        w_transposes(1, psm, "mx")
         w_copy(1, 0, scopy)
         w_copy(1, 1, vcopy)
         x_transposes(0)
         x_copy(0, scopy)
         w_quant(1)
-        w_transposes(3, ("l1", "l3"))
-        x_quant(0)
+        w_transposes(3, psl, "l")
         w_copy(3, 0, scopy)
+        z_quant(-2)
         w_copy(3, 1, vcopy)
         xa_transposes(0)
-        b_transposes()
-        x_transposes(1)
         xa_copy(0, scopy)
-        w_quant(3)
-        vcopy(out=bT[:], in_=bbank[0][:])
+        b_transposes()
         mx_pass(1, 0)
-        mx_pass(3, 0)
-        x_copy(1, scopy)
+        x_transposes(1)
+        vcopy(out=bT[:], in_=bbank[0][:])
         mx_out(1, 0)
-        x_quant(1)
-        mx_out(3, 0)
+        w_quant(3)
         lora(1, 0)
-        lora(3, 0)
-        mx_pass(1, 1)
-        mx_pass(3, 1)
-        x_transposes(2)
+        x_copy(1, scopy)
+        x_transposes(2, "gt")
         xa_transposes(1)
+        mx_pass(3, 0)
+        lora(3, 0)
+        z_quant(-1)
+        x_copy(2, scopy)
+        xa_copy(1, scopy)
+        mx_pass(1, 1)
+        add(1, 0)
+        mx_out(3, 0)
+        silu(0)
+        lora(1, 1)
+        xa_transposes(2)
+        x_transposes(3)
+        mx_pass(1, 2)
+        mx_out(1, 1)
+        mx_pass(3, 1)
 
-        for t in range(NT):
-            q, r = divmod(t, 2)
-            if r == 1:
-                x_transposes(q + 3)
-                xa_transposes(q + 2)
-                g_transposes(q - 1)
-            add(1, t)
-            mx_out(1, t + 1)
-            lora(1, t + 1)
-            mx_pass(1, t + 2)
-            add(3, t)
-            silu(t)
-            mx_out(3, t + 1)
-            lora(3, t + 1)
-            if t == 2:
-                a2_transposes()
-                a2_copy()
-            if t == 3:
+        for q in range(NQ):
+            a, b, a2, b2, a4 = 2 * q, 2 * q + 1, 2 * q + 2, 2 * q + 3, 2 * q + 4
+            z_quant(q)
+            if q == 2:
                 a2_quant()
-            if r == 0:
-                g_quant(q - 2)
-                x_copy(q + 2, vcopy)
-                xa_copy(q + 1, scopy)
-                ga2(q - 2)
-            else:
-                g_copy(q - 1, vcopy)
-                x_quant(q + 2)
-                o_out(q - 2)
-            mx_pass(3, t + 2)
-            gate(t)
-            if t == NT - 1:
-                last_transposes(NT - 2, "x")
+            mx_out(1, a2)
+            if q > 0:
+                xa_transposes(q + 2)
+            g_transposes(q - 2)
+            if q == 1:
+                a2_transposes()
+            gate(a - 1)
+            add(3, a)
+            gate(a)
+            xa_copy(q + 2, vcopy)
+            lora(1, a2)
+            mx_pass(3, a2)
+            mx_out(3, b)
+            if q < NQ - 1:
+                g_cast(q - 1)
+            ga2(q - 3)
+            mx_pass(1, b2)
+            add(1, b)
+            x_copy(q + 3, scopy)
+            lora(3, b)
+            g_copy(q - 2, vcopy)
+            if q == 1:
+                a2_copy()
+            mx_out(3, a2)
+            silu(b)
+            add(1, a2)
+            x_transposes(q + 4)
+            lora(3, a2)
+            mx_pass(1, a4)
+            mx_out(1, b2)
+            o_out(q - 3)
+            silu(a2)
+            add(3, b)
+            lora(1, b2)
+            mx_pass(3, b2)
 
-        last_copy(NT - 2, scopy)
-        g_quant(NQ - 2)
-        last_transposes(NT - 1, "xa")
-        last_quant(NT - 2)
+        t = NT - 1
+        last_transposes(t - 1)
+        g_cast(NQ - 2)
+        z_quant(NQ)
+        gate(t)
+        g_transposes(NQ - 2)
+        last_transposes(t)
+        last_copy(t - 1, scopy)
+        ga2(NQ - 3)
+        g_copy(NQ - 2, vcopy)
+        last_copy(t, scopy)
+        last_quant(t - 1)
+        z_quant(NQ + 1)
+        last_quant(t)
+        o_out(NQ - 3)
+        last_out(t - 1, scopy)
         ga2(NQ - 2)
+        last_out(t, scopy)
         o_out(NQ - 2)
-        last_copy(NT - 1, vcopy)
-        last_quant(NT - 1)
-        last_out(NT - 2, "x")
-        last_out(NT - 1, "xa")

@@ -319,16 +319,21 @@ def tile_feedforward_pa_t_kernel(
             if j == 1:
                 store_g(q)
 
-        def g_cast(q):
+        def g_cast_a(q):
             if not 0 <= q < NQ - 1:
                 return
             gb_sb[q] = rot2.tile([P, 2 * F], BF16, name="gb_sb", tag="gb_sb")
+            vcopy(out=gb_sb[q][:, 0:F], in_=g_sb[q][:, 0:F])
+
+        def g_cast_b(q):
+            if not 0 <= q < NQ - 1:
+                return
             if q == NQ - 2:
-                scopy(out=gb_sb[q][:], in_=g_sb[q][:])
+                scopy(out=gb_sb[q][:, F : 2 * F], in_=g_sb[q][:, F : 2 * F])
                 return
             nc.gpsimd.tensor_scalar(
-                out=gb_sb[q][:],
-                in0=g_sb[q][:],
+                out=gb_sb[q][:, F : 2 * F],
+                in0=g_sb[q][:, F : 2 * F],
                 scalar1=1.0,
                 scalar2=0.0,
                 op0=ALU.mult,
@@ -372,7 +377,7 @@ def tile_feedforward_pa_t_kernel(
             if not 0 <= q < NQ - 1:
                 return
             o_sb = rot2.tile([P, 2 * R], F32, name="o_sb", tag="o_sb")
-            vcopy(out=o_sb[:], in_=obank[q][:, 0:2, :].rearrange("p j r -> p (j r)"))
+            scopy(out=o_sb[:], in_=obank[q][:, 0:2, :].rearrange("p j r -> p (j r)"))
             nc.sync.dma_start(out=ov[:, 2 * R * q : 2 * R * (q + 1)], in_=o_sb[:])
 
         def last_transposes(t):
@@ -454,6 +459,7 @@ def tile_feedforward_pa_t_kernel(
         for q in range(NQ):
             a, b, a2, b2, a4 = 2 * q, 2 * q + 1, 2 * q + 2, 2 * q + 3, 2 * q + 4
             z_quant(q)
+            g_cast_a(q - 1)
             if q == 2:
                 a2_quant()
             mx_out(1, a2)
@@ -465,17 +471,16 @@ def tile_feedforward_pa_t_kernel(
             gate(a - 1)
             add(3, a)
             gate(a)
-            xa_copy(q + 2, vcopy)
             lora(1, a2)
             mx_pass(3, a2)
             mx_out(3, b)
             if q < NQ - 1:
-                g_cast(q - 1)
-            ga2(q - 3)
+                g_cast_b(q - 1)
             mx_pass(1, b2)
             add(1, b)
             x_copy(q + 3, scopy)
             lora(3, b)
+            xa_copy(q + 2, vcopy)
             g_copy(q - 2, vcopy)
             if q == 1:
                 a2_copy()
@@ -483,6 +488,7 @@ def tile_feedforward_pa_t_kernel(
             silu(b)
             add(1, a2)
             x_transposes(q + 4)
+            ga2(q - 3)
             lora(3, a2)
             mx_pass(1, a4)
             mx_out(1, b2)
@@ -494,7 +500,7 @@ def tile_feedforward_pa_t_kernel(
 
         t = NT - 1
         last_transposes(t - 1)
-        g_cast(NQ - 2)
+        g_cast_b(NQ - 2)
         z_quant(NQ)
         gate(t)
         g_transposes(NQ - 2)

@@ -73,7 +73,6 @@ def tile_feedforward_pa_t_kernel(
         load_w(1, w1)
         nc.sync.dma_start(out=x_sb[0][:, 0 : 2 * D], in_=xv[:, 0 : 2 * D])
         load_w(3, w3)
-        load_xa(0)
         nc.sync.dma_start(
             out=b_sb[:, 0 : 4 * R].rearrange("p (c r) -> p c r", c=4),
             in_=lora_B1.rearrange("(c p) r -> p c r", p=P),
@@ -82,6 +81,7 @@ def tile_feedforward_pa_t_kernel(
             out=b_sb[:, 4 * R : 8 * R].rearrange("p (c r) -> p c r", c=4),
             in_=lora_B3.rearrange("(c p) r -> p c r", p=P),
         )
+        load_xa(0)
         nc.sync.dma_start(out=x_sb[0][:, 2 * D : 4 * D], in_=xv[:, 2 * D : 4 * D])
         for h in range(2):
             nc.sync.dma_start(
@@ -123,10 +123,9 @@ def tile_feedforward_pa_t_kernel(
             wc[k] = keep.tile([P, F], U32, name="wc%d" % k, align_bytes=64)
             ws[k] = keep.tile([P, F], U8, name="ws%d" % k, align_bytes=64)
 
-        def w_transposes(k, pool, tag):
-            for h in range(2):
-                wbank[(k, h)] = pool.tile([P, 2, 2, P], F32, name="wbank", tag=tag)
-                word_transposes(w_sb[k][:].bitcast(F32)[:, 512 * h : 512 * h + 512], wbank[(k, h)])
+        def w_transposes(k, pool, tag, h):
+            wbank[(k, h)] = pool.tile([P, 2, 2, P], F32, name="wbank", tag=tag)
+            word_transposes(w_sb[k][:].bitcast(F32)[:, 512 * h : 512 * h + 512], wbank[(k, h)])
 
         def w_copy(k, h, copy):
             word_copy(copy, wg[k][:].bitcast(F32)[:, 512 * h : 512 * h + 512], wbank[(k, h)])
@@ -268,11 +267,12 @@ def tile_feedforward_pa_t_kernel(
                 stop=True,
             )
 
-        def mx_out(k, t):
+        def mx_out(k, t, copy=None):
+            copy = copy or scopy
             if not ok(t):
                 return
             m_sb[(k, t)] = rot3.tile([P, F], F32, name="m%d" % k, tag="m%d" % k)
-            scopy(out=m_sb[(k, t)][:], in_=mx[(k, t)][:])
+            copy(out=m_sb[(k, t)][:], in_=mx[(k, t)][:])
 
         def add(k, t):
             if not ok(t):
@@ -365,7 +365,7 @@ def tile_feedforward_pa_t_kernel(
         def ga2(q):
             if not 0 <= q < NQ - 1:
                 return
-            if q < NQ - 3:
+            if q < NQ - 4:
                 obank[q] = ps1.tile([P, 4, R], F32, name="obank", tag="xo")
             else:
                 obank[q] = psl.tile([P, 4, R], F32, name="obank", tag="l")
@@ -373,11 +373,11 @@ def tile_feedforward_pa_t_kernel(
                 cols = slice(P * j, P * (j + 1))
                 ga2_pass(obank[q][:, j, :], gc[q][:, cols], gs[q][:, cols])
 
-        def o_out(q):
+        def o_out(q, copy):
             if not 0 <= q < NQ - 1:
                 return
-            o_sb = rot2.tile([P, 2 * R], F32, name="o_sb", tag="o_sb")
-            scopy(out=o_sb[:], in_=obank[q][:, 0:2, :].rearrange("p j r -> p (j r)"))
+            o_sb = rot4.tile([P, 2 * R], F32, name="o_sb", tag="o_sb")
+            copy(out=o_sb[:], in_=obank[q][:, 0:2, :].rearrange("p j r -> p (j r)"))
             nc.sync.dma_start(out=ov[:, 2 * R * q : 2 * R * (q + 1)], in_=o_sb[:])
 
         def last_transposes(t):
@@ -418,43 +418,47 @@ def tile_feedforward_pa_t_kernel(
         dummy = keep.tile([P, 1], F32, name="dummy")
         nc.scalar.activation(out=dummy[:], in_=ident_f[:, 0:1], func=ACT.Silu)
 
-        w_transposes(1, psm, "mx")
+        w_transposes(1, psm, "mx", 0)
+        w_transposes(1, psm, "mx", 1)
         w_copy(1, 0, scopy)
         w_copy(1, 1, vcopy)
         x_transposes(0)
         x_copy(0, scopy)
         w_quant(1)
-        w_transposes(3, psl, "l")
+        w_transposes(3, psl, "l", 0)
+        w_transposes(3, psl, "l", 1)
         w_copy(3, 0, scopy)
         z_quant(-2)
         w_copy(3, 1, vcopy)
-        xa_transposes(0)
-        xa_copy(0, scopy)
         b_transposes()
         mx_pass(1, 0)
-        x_transposes(1)
+        xa_transposes(0)
+        xa_copy(0, scopy)
         vcopy(out=bT[:], in_=bbank[0][:])
-        mx_out(1, 0)
         w_quant(3)
-        lora(1, 0)
+        mx_out(1, 0, vcopy)
+        x_transposes(1)
         x_copy(1, scopy)
-        x_transposes(2, "gt")
-        xa_transposes(1)
-        mx_pass(3, 0)
-        lora(3, 0)
-        z_quant(-1)
-        x_copy(2, scopy)
-        xa_copy(1, scopy)
         mx_pass(1, 1)
+        lora(1, 0)
+        mx_out(1, 1)
+        x_transposes(2, "gt")
+        x_copy(2, scopy)
+        xa_transposes(1)
         add(1, 0)
+        z_quant(-1)
+        xa_copy(1, vcopy)
+        mx_pass(3, 0)
+        lora(1, 1)
+        lora(3, 0)
+        add(1, 1)
         mx_out(3, 0)
         silu(0)
-        lora(1, 1)
-        xa_transposes(2)
-        x_transposes(3)
         mx_pass(1, 2)
-        mx_out(1, 1)
+        lora(1, 2)
+        x_transposes(3)
         mx_pass(3, 1)
+        xa_transposes(2)
 
         for q in range(NQ):
             a, b, a2, b2, a4 = 2 * q, 2 * q + 1, 2 * q + 2, 2 * q + 3, 2 * q + 4
@@ -471,15 +475,17 @@ def tile_feedforward_pa_t_kernel(
             gate(a - 1)
             add(3, a)
             gate(a)
-            lora(1, a2)
+            if q > 0:
+                lora(1, a2)
             mx_pass(3, a2)
             mx_out(3, b)
             if q < NQ - 1:
                 g_cast_b(q - 1)
-            mx_pass(1, b2)
-            add(1, b)
-            x_copy(q + 3, scopy)
             lora(3, b)
+            mx_pass(1, b2)
+            if q > 0:
+                add(1, b)
+            x_copy(q + 3, scopy)
             xa_copy(q + 2, vcopy)
             g_copy(q - 2, vcopy)
             if q == 1:
@@ -492,7 +498,8 @@ def tile_feedforward_pa_t_kernel(
             lora(3, a2)
             mx_pass(1, a4)
             mx_out(1, b2)
-            o_out(q - 3)
+            if q < NQ - 1:
+                o_out(q - 3, vcopy if q % 3 == 0 else scopy)
             silu(a2)
             add(3, b)
             lora(1, b2)
@@ -505,15 +512,16 @@ def tile_feedforward_pa_t_kernel(
         gate(t)
         g_transposes(NQ - 2)
         last_transposes(t)
-        last_copy(t - 1, scopy)
         ga2(NQ - 3)
+        o_out(NQ - 4, vcopy)
+        last_copy(t - 1, scopy)
         g_copy(NQ - 2, vcopy)
         last_copy(t, scopy)
+        o_out(NQ - 3, scopy)
         last_quant(t - 1)
         z_quant(NQ + 1)
         last_quant(t)
-        o_out(NQ - 3)
         last_out(t - 1, scopy)
         ga2(NQ - 2)
+        o_out(NQ - 2, vcopy)
         last_out(t, scopy)
-        o_out(NQ - 2)

@@ -59,7 +59,7 @@ def tile_feedforward_pa_t_kernel(
             for h in range(2):
                 nc.sync.dma_start(
                     out=w_sb[k][:, 2 * D * h : 2 * D * (h + 1)].rearrange("p (c d) -> p c d", c=2),
-                    in_=w[2 * P * h : 2 * P * (h + 1), :].rearrange("(c p) d -> p c d", p=P),
+                    in_=w[2 * P * h : 2 * P * (h + 1), :].rearrange("(p c) d -> p c d", c=2),
                 )
 
         def load_x(g):
@@ -75,11 +75,11 @@ def tile_feedforward_pa_t_kernel(
         load_w(3, w3)
         nc.sync.dma_start(
             out=b_sb[:, 0 : 4 * R].rearrange("p (c r) -> p c r", c=4),
-            in_=lora_B1.rearrange("(c p) r -> p c r", p=P),
+            in_=lora_B1.rearrange("(p c) r -> p c r", c=4),
         )
         nc.sync.dma_start(
             out=b_sb[:, 4 * R : 8 * R].rearrange("p (c r) -> p c r", c=4),
-            in_=lora_B3.rearrange("(c p) r -> p c r", p=P),
+            in_=lora_B3.rearrange("(p c) r -> p c r", c=4),
         )
         load_xa(0)
         nc.sync.dma_start(out=x_sb[0][:, 2 * D : 4 * D], in_=xv[:, 2 * D : 4 * D])
@@ -128,7 +128,12 @@ def tile_feedforward_pa_t_kernel(
             word_transposes(w_sb[k][:].bitcast(F32)[:, 512 * h : 512 * h + 512], wbank[(k, h)])
 
         def w_copy(k, h, copy):
-            word_copy(copy, wg[k][:].bitcast(F32)[:, 512 * h : 512 * h + 512], wbank[(k, h)])
+            copy(
+                out=wg[k][:].bitcast(F32)[:, 512 * h : 512 * h + 512].rearrange(
+                    "p (r a u) -> p r a u", a=2, u=2
+                ),
+                in_=wbank[(k, h)][:].rearrange("p a u r -> p r a u"),
+            )
 
         def w_quant(k):
             nc.vector.quantize_mx(out=wc[k][:].bitcast(FP8X4), scales=ws[k][:], in_=wg[k][:])
@@ -201,6 +206,12 @@ def tile_feedforward_pa_t_kernel(
                 nc.tensor.transpose(
                     bbank[0][:, P * i : P * (i + 1)], b_sb[:, R * i : R * (i + 1)], ident_b[:]
                 )
+
+        def b_copy(b, copy):
+            copy(
+                out=bT[:, F * b : F * (b + 1)].rearrange("p (f c) -> p f c", c=4),
+                in_=bbank[0][:, F * b : F * (b + 1)].rearrange("p (c f) -> p f c", c=4),
+            )
 
         ag = keep.tile([P, 4 * R], BF16, name="ag", align_bytes=64)
         ac = keep.tile([P, R], U32, name="ac", align_bytes=64)
@@ -433,13 +444,14 @@ def tile_feedforward_pa_t_kernel(
         b_transposes()
         mx_pass(1, 0)
         xa_transposes(0)
-        xa_copy(0, scopy)
-        vcopy(out=bT[:], in_=bbank[0][:])
+        b_copy(0, scopy)
         w_quant(3)
-        mx_out(1, 0, vcopy)
+        xa_copy(0, vcopy)
+        b_copy(1, scopy)
+        mx_out(1, 0)
+        mx_pass(1, 1)
         x_transposes(1)
         x_copy(1, scopy)
-        mx_pass(1, 1)
         lora(1, 0)
         mx_out(1, 1)
         x_transposes(2, "gt")

@@ -37,9 +37,9 @@ def tile_feedforward_pa_t_kernel(
     with ExitStack() as ctx:
         ctx.enter_context(tc.manual_schedule())
         keep = ctx.enter_context(tc.tile_pool(name="keep", bufs=1))
-        rot2 = ctx.enter_context(tc.tile_pool(name="rot2", bufs=2))
-        rot4 = ctx.enter_context(tc.tile_pool(name="rot4", bufs=4))
-        rot3 = ctx.enter_context(tc.tile_pool(name="rot3", bufs=3))
+        rot2 = ctx.enter_context(tc.tile_pool(name="rot2", bufs=4))
+        rot4 = ctx.enter_context(tc.tile_pool(name="rot4", bufs=6))
+        rot3 = ctx.enter_context(tc.tile_pool(name="rot3", bufs=6))
         ps1 = ctx.enter_context(tc.psum_pool(name="ps1", bufs=1))
         psm = ctx.enter_context(tc.psum_pool(name="psm", bufs=2))
         psl = ctx.enter_context(tc.psum_pool(name="psl", bufs=3))
@@ -487,14 +487,14 @@ def tile_feedforward_pa_t_kernel(
             gate(a - 1)
             add(3, a)
             gate(a)
+            mx_pass(3, a2)
             if q > 0:
                 lora(1, a2)
-            mx_pass(3, a2)
             mx_out(3, b)
             if q < NQ - 1:
                 g_cast_b(q - 1)
-            lora(3, b)
             mx_pass(1, b2)
+            lora(3, b)
             if q > 0:
                 add(1, b)
             x_copy(q + 3, scopy)
@@ -507,15 +507,15 @@ def tile_feedforward_pa_t_kernel(
             add(1, a2)
             x_transposes(q + 4)
             ga2(q - 3)
-            lora(3, a2)
             mx_pass(1, a4)
+            lora(3, a2)
             mx_out(1, b2)
             if q < NQ - 1:
                 o_out(q - 3, vcopy if q % 3 == 0 else scopy)
             silu(a2)
             add(3, b)
-            lora(1, b2)
             mx_pass(3, b2)
+            lora(1, b2)
 
         t = NT - 1
         last_transposes(t - 1)

@@ -334,17 +334,17 @@ def tile_feedforward_pa_t_kernel(
             if not 0 <= q < NQ - 1:
                 return
             gb_sb[q] = rot2.tile([P, 2 * F], BF16, name="gb_sb", tag="gb_sb")
-            vcopy(out=gb_sb[q][:, 0:F], in_=g_sb[q][:, 0:F])
+            vcopy(out=gb_sb[q][:, 0:384], in_=g_sb[q][:, 0:384])
 
         def g_cast_b(q):
             if not 0 <= q < NQ - 1:
                 return
             if q == NQ - 2:
-                scopy(out=gb_sb[q][:, F : 2 * F], in_=g_sb[q][:, F : 2 * F])
+                scopy(out=gb_sb[q][:, 384 : 2 * F], in_=g_sb[q][:, 384 : 2 * F])
                 return
             nc.gpsimd.tensor_scalar(
-                out=gb_sb[q][:, F : 2 * F],
-                in0=g_sb[q][:, F : 2 * F],
+                out=gb_sb[q][:, 384 : 2 * F],
+                in0=g_sb[q][:, 384 : 2 * F],
                 scalar1=1.0,
                 scalar2=0.0,
                 op0=ALU.mult,
@@ -422,26 +422,36 @@ def tile_feedforward_pa_t_kernel(
 
         warm = keep.tile([P, F], BF16, name="warm")
         nc.vector.memset(warm[:], 0.0)
-        wps = ps1.tile([P, F], F32, name="wps", tag="gt")
-        for i in range(WARM):
-            nc.tensor.matmul(out=wps[:], lhsT=warm[:, 0:P], rhs=warm[:], start=True, stop=True)
+        wps = ps1.tile([P, F], F32, name="wps", tag="xo")
+
+        def keep_warm(n=1):
+            for i in range(n):
+                nc.tensor.matmul(out=wps[:], lhsT=warm[:, 0:P], rhs=warm[:], start=True, stop=True)
+
+        keep_warm(WARM)
 
         dummy = keep.tile([P, 1], F32, name="dummy")
         nc.scalar.activation(out=dummy[:], in_=ident_f[:, 0:1], func=ACT.Silu)
 
         w_transposes(1, psm, "mx", 0)
+        keep_warm()
         w_transposes(1, psm, "mx", 1)
+        keep_warm()
         w_copy(1, 0, scopy)
         w_copy(1, 1, vcopy)
         x_transposes(0)
+        keep_warm()
         x_copy(0, scopy)
         w_quant(1)
         w_transposes(3, psl, "l", 0)
+        keep_warm()
         w_transposes(3, psl, "l", 1)
+        keep_warm()
         w_copy(3, 0, scopy)
         z_quant(-2)
         w_copy(3, 1, vcopy)
         b_transposes()
+        keep_warm()
         mx_pass(1, 0)
         xa_transposes(0)
         b_copy(0, scopy)

@@ -434,13 +434,11 @@ def tile_feedforward_pa_t_kernel(
         nc.scalar.activation(out=dummy[:], in_=ident_f[:, 0:1], func=ACT.Silu)
 
         w_transposes(1, psm, "mx", 0)
-        keep_warm()
         w_transposes(1, psm, "mx", 1)
         keep_warm()
         w_copy(1, 0, scopy)
         w_copy(1, 1, vcopy)
         x_transposes(0)
-        keep_warm()
         x_copy(0, scopy)
         w_quant(1)
         w_transposes(3, psl, "l", 0)
@@ -451,7 +449,6 @@ def tile_feedforward_pa_t_kernel(
         z_quant(-2)
         w_copy(3, 1, vcopy)
         b_transposes()
-        keep_warm()
         mx_pass(1, 0)
         xa_transposes(0)
         b_copy(0, scopy)
@@ -528,6 +525,9 @@ def tile_feedforward_pa_t_kernel(
             lora(1, b2)
 
         t = NT - 1
+        wps_end = ps1.tile([P, F], F32, name="wps_end", tag="xo")
+        for i in range(3):
+            nc.tensor.matmul(out=wps_end[:], lhsT=warm[:, 0:P], rhs=warm[:], start=True, stop=True)
         last_transposes(t - 1)
         g_cast_b(NQ - 2)
         z_quant(NQ)

@@ -504,7 +504,7 @@ def tile_feedforward_pa_t_kernel(
             lora(3, b)
             if q > 0:
                 add(1, b)
-            x_copy(q + 3, scopy)
+            x_copy(q + 3, vcopy if q == 0 else scopy)
             xa_copy(q + 2, vcopy)
             g_copy(q - 2, vcopy)
             if q == 1:

from contextlib import ExitStack

import concourse.mybir as mybir
from concourse.masks import make_identity

F32 = mybir.dt.float32
BF16 = mybir.dt.bfloat16
U32 = mybir.dt.uint32
U8 = mybir.dt.uint8
FP8X4 = mybir.dt.float8_e4m3fn_x4
ACT = mybir.ActivationFunctionType
ALU = mybir.AluOpType

P = 128
TOKENS = 4096
D = 512
F = 512
R = 128
NT = TOKENS // P
NQ = NT // 2
TPG = 4
NG = NT // TPG
WARM = 5
FLOPS = 2 * TOKENS * (2 * D * F + 2 * R * F + F * R)


def tile_feedforward_pa_t_kernel(
    tc, x, w1, w3, xa1, xa3, lora_B1, lora_B3, lora_A2, out_0, out_1
):
    nc = tc.nc
    xv = x.flatten_outer_dims().rearrange("(p j) d -> p (j d)", j=NT)
    xa1v = xa1.flatten_outer_dims().rearrange("(p j) r -> p (j r)", j=NT)
    xa3v = xa3.flatten_outer_dims().rearrange("(p j) r -> p (j r)", j=NT)
    gv = out_0.flatten_outer_dims().rearrange("(p j) f -> p (j f)", j=NT)
    ov = out_1.flatten_outer_dims().rearrange("(p j) r -> p (j r)", j=NT)

    with ExitStack() as ctx:
        ctx.enter_context(tc.manual_schedule())
        keep = ctx.enter_context(tc.tile_pool(name="keep", bufs=1))
        rot2 = ctx.enter_context(tc.tile_pool(name="rot2", bufs=4))
        rot4 = ctx.enter_context(tc.tile_pool(name="rot4", bufs=6))
        rot3 = ctx.enter_context(tc.tile_pool(name="rot3", bufs=6))
        ps1 = ctx.enter_context(tc.psum_pool(name="ps1", bufs=1))
        psm = ctx.enter_context(tc.psum_pool(name="psm", bufs=2))
        psl = ctx.enter_context(tc.psum_pool(name="psl", bufs=3))

        w_sb = {}
        for k in (1, 3):
            w_sb[k] = keep.tile([P, 4 * D], BF16, name="w_sb%d" % k)
        b_sb = keep.tile([P, 2 * 4 * R], BF16, name="b_sb")
        a_sb = keep.tile([P, F], BF16, name="a_sb")
        x_sb = {}
        xa_sb = {}
        for g in range(NG):
            x_sb[g] = keep.tile([P, TPG * D], BF16, name="x_sb%d" % g)
            xa_sb[g] = keep.tile([P, 2 * TPG * R], BF16, name="xa_sb%d" % g)

        def load_w(k, w):
            for h in range(2):
                nc.sync.dma_start(
                    out=w_sb[k][:, 2 * D * h : 2 * D * (h + 1)].rearrange("p (c d) -> p c d", c=2),
                    in_=w[2 * P * h : 2 * P * (h + 1), :].rearrange("(p c) d -> p c d", c=2),
                )

        def load_x(g):
            nc.sync.dma_start(out=x_sb[g][:], in_=xv[:, TPG * D * g : TPG * D * (g + 1)])

        def load_xa(g):
            n = TPG * R
            nc.sync.dma_start(out=xa_sb[g][:, 0:n], in_=xa1v[:, n * g : n * (g + 1)])
            nc.sync.dma_start(out=xa_sb[g][:, n : 2 * n], in_=xa3v[:, n * g : n * (g + 1)])

        load_w(1, w1)
        nc.sync.dma_start(out=x_sb[0][:, 0 : 2 * D], in_=xv[:, 0 : 2 * D])
        load_w(3, w3)
        nc.sync.dma_start(
            out=b_sb[:, 0 : 4 * R].rearrange("p (c r) -> p c r", c=4),
            in_=lora_B1.rearrange("(p c) r -> p c r", c=4),
        )
        nc.sync.dma_start(
            out=b_sb[:, 4 * R : 8 * R].rearrange("p (c r) -> p c r", c=4),
            in_=lora_B3.rearrange("(p c) r -> p c r", c=4),
        )
        load_xa(0)
        nc.sync.dma_start(out=x_sb[0][:, 2 * D : 4 * D], in_=xv[:, 2 * D : 4 * D])
        for h in range(2):
            nc.sync.dma_start(
                out=x_sb[1][:, 2 * D * h : 2 * D * (h + 1)],
                in_=xv[:, 2 * D * (h + 2) : 2 * D * (h + 3)],
            )
        load_xa(1)
        nc.sync.dma_start(out=a_sb[:], in_=lora_A2)
        for g in range(2, NG):
            load_x(g)
            load_xa(g)

        ident_f = keep.tile([P, P], F32, name="ident_f")
        make_identity(nc, ident_f[:])
        ident_b = keep.tile([P, P], BF16, name="ident_b")
        make_identity(nc, ident_b[:])

        vcopy = nc.vector.tensor_copy
        scopy = nc.scalar.copy

        def word_transposes(words, bank):
            for a in range(2):
                for u in range(2):
                    c0 = 256 * a + 128 * u
                    nc.tensor.transpose(bank[:, a, u, :], words[:, c0 : c0 + 128], ident_f[:])

        def word_copy(copy, words, bank):
            copy(
                out=words.rearrange("p (a r u) -> p a r u", a=2, u=2),
                in_=bank[:].rearrange("p a u r -> p a r u"),
            )

        wg = {}
        wc = {}
        ws = {}
        wbank = {}
        for k in (1, 3):
            wg[k] = keep.tile([P, 4 * F], BF16, name="wg%d" % k, align_bytes=64)
            wc[k] = keep.tile([P, F], U32, name="wc%d" % k, align_bytes=64)
            ws[k] = keep.tile([P, F], U8, name="ws%d" % k, align_bytes=64)

        def w_transposes(k, pool, tag, h):
            wbank[(k, h)] = pool.tile([P, 2, 2, P], F32, name="wbank", tag=tag)
            word_transposes(w_sb[k][:].bitcast(F32)[:, 512 * h : 512 * h + 512], wbank[(k, h)])

        def w_copy(k, h, copy):
            copy(
                out=wg[k][:].bitcast(F32)[:, 512 * h : 512 * h + 512].rearrange(
                    "p (r a u) -> p r a u", a=2, u=2
                ),
                in_=wbank[(k, h)][:].rearrange("p a u r -> p r a u"),
            )

        def w_quant(k):
            nc.vector.quantize_mx(out=wc[k][:].bitcast(FP8X4), scales=ws[k][:], in_=wg[k][:])

        gc = {}
        gs = {}
        xc = {}
        xs = {}
        xaT = {}
        xbank = {}
        abank = {}
        zg = {}

        def z_half(q, part):
            if q not in zg:
                zg[q] = rot3.tile([P, 16 * P], BF16, name="zg", tag="zg", align_bytes=64)
            return zg[q][:, 8 * P * part : 8 * P * (part + 1)]

        def z_quant(q):
            lo, hi = (1 if q < 3 else 0), (1 if q + 2 >= NQ else 2)
            if hi <= lo:
                return
            zc = rot4.tile([P, 4 * P], U32, name="zc", tag="zc", align_bytes=64)
            zs = rot4.tile([P, 4 * P], U8, name="zs", tag="zs", align_bytes=64)
            nc.vector.quantize_mx(
                out=zc[:, 2 * P * lo : 2 * P * hi].bitcast(FP8X4),
                scales=zs[:, 2 * P * lo : 2 * P * hi],
                in_=zg[q][:, 8 * P * lo : 8 * P * hi],
            )
            gc[q - 3], gs[q - 3] = zc[:, 0 : 2 * P], zs[:, 0 : 2 * P]
            xc[q + 2], xs[q + 2] = zc[:, 2 * P : 4 * P], zs[:, 2 * P : 4 * P]

        def x_transposes(q, tag="x"):
            if not 0 <= q < NQ:
                return
            g, h = divmod(q, 2)
            xbank[q] = ps1.tile([P, 2, 2, P], F32, name="xbank", tag=tag)
            word_transposes(x_sb[g][:].bitcast(F32)[:, 512 * h : 512 * h + 512], xbank[q])

        def x_copy(q, copy):
            if not 0 <= q < NQ:
                return
            word_copy(copy, z_half(q - 2, 1).bitcast(F32), xbank[q])

        def xa_transposes(q):
            if not 0 <= q < NQ:
                return
            g, h = divmod(q, 2)
            abank[q] = ps1.tile([P, 8 * P], BF16, name="abank", tag="xo")
            for b in range(2):
                for j in range(2):
                    i = TPG * b + 2 * h + j
                    n = 2 * b + j
                    nc.tensor.transpose(
                        abank[q][:, P * n : P * (n + 1)], xa_sb[g][:, R * i : R * (i + 1)], ident_b[:]
                    )

        def xa_copy(q, copy):
            if not 0 <= q < NQ:
                return
            xaT[q] = rot3.tile([P, 4 * P], BF16, name="xaT", tag="xaT")
            copy(out=xaT[q][:], in_=abank[q][:, 0 : 4 * P])

        bT = keep.tile([P, 2 * F], BF16, name="bT")
        bbank = {}

        def b_transposes():
            bbank[0] = ps1.tile([P, 2 * F], BF16, name="bbank", tag="gt")
            for i in range(8):
                nc.tensor.transpose(
                    bbank[0][:, P * i : P * (i + 1)], b_sb[:, R * i : R * (i + 1)], ident_b[:]
                )

        def b_copy(b, copy):
            copy(
                out=bT[:, F * b : F * (b + 1)].rearrange("p (f c) -> p f c", c=4),
                in_=bbank[0][:, F * b : F * (b + 1)].rearrange("p (c f) -> p f c", c=4),
            )

        ag = keep.tile([P, 4 * R], BF16, name="ag", align_bytes=64)
        ac = keep.tile([P, R], U32, name="ac", align_bytes=64)
        asc = keep.tile([P, R], U8, name="asc", align_bytes=64)
        a2bank = {}

        def a2_transposes():
            a2bank[0] = ps1.tile([P, 4, P], F32, name="a2bank", tag="gt")
            for u in range(2):
                nc.tensor.transpose(
                    a2bank[0][:, u, :], a_sb[:].bitcast(F32)[:, P * u : P * (u + 1)], ident_f[:]
                )

        def a2_copy():
            vcopy(
                out=ag[:].bitcast(F32).rearrange("p (r u) -> p r u", u=2),
                in_=a2bank[0][:, 0:2, :].rearrange("p u r -> p r u"),
            )

        def a2_quant():
            nc.vector.quantize_mx(out=ac[:].bitcast(FP8X4), scales=asc[:], in_=ag[:])

        mx = {}
        lo = {}
        m_sb = {}
        h_sb = {}
        s_sb = {}
        g_sb = {}
        gb_sb = {}
        gbank = {}
        gg = {}
        obank = {}

        def ok(t):
            return 0 <= t < NT

        def mx_pass(k, t):
            if not ok(t):
                return
            q, j = divmod(t, 2)
            mx[(k, t)] = psm.tile([P, F], F32, name="mx", tag="mx")
            nc.tensor.matmul_mx(
                out=mx[(k, t)][:],
                lhsT=xc[q][:, P * j : P * (j + 1)].bitcast(FP8X4),
                lhsT_scale=xs[q][:, P * j : P * (j + 1)],
                rhs=wc[k][:].bitcast(FP8X4),
                rhs_scale=ws[k][:],
                start=True,
                stop=True,
            )

        def lora(k, t):
            if not ok(t):
                return
            q, j = divmod(t, 2)
            b = 0 if k == 1 else 1
            n = 2 * b + j
            lo[(k, t)] = psl.tile([P, F], F32, name="lo", tag="l")
            nc.tensor.matmul(
                out=lo[(k, t)][:],
                lhsT=xaT[q][:, P * n : P * (n + 1)],
                rhs=bT[:, F * b : F * (b + 1)],
                start=True,
                stop=True,
            )

        def mx_out(k, t, copy=None):
            copy = copy or scopy
            if not ok(t):
                return
            m_sb[(k, t)] = rot3.tile([P, F], F32, name="m%d" % k, tag="m%d" % k)
            copy(out=m_sb[(k, t)][:], in_=mx[(k, t)][:])

        def add(k, t):
            if not ok(t):
                return
            h_sb[(k, t)] = rot3.tile([P, F], F32, name="h%d" % k, tag="h%d" % k)
            nc.vector.scalar_tensor_tensor(
                out=h_sb[(k, t)][:],
                in0=lo[(k, t)][:],
                scalar=2.0,
                in1=m_sb[(k, t)][:],
                op0=ALU.mult,
                op1=ALU.add,
            )

        def silu(t):
            if not ok(t):
                return
            s_sb[t] = rot3.tile([P, F], F32, name="s1", tag="s1")
            nc.scalar.activation(out=s_sb[t][:], in_=h_sb[(1, t)][:], func=ACT.Silu)

        def product(engine, t, c0, c1):
            j = t % 2
            engine.tensor_tensor(
                out=g_sb[t // 2][:, F * j + c0 : F * j + c1],
                in0=s_sb[t][:, c0:c1],
                in1=h_sb[(3, t)][:, c0:c1],
                op=ALU.mult,
            )

        def store_g(q):
            nc.sync.dma_start(out=gv[:, 2 * F * q : 2 * F * (q + 1)], in_=g_sb[q][:])

        def gate(t):
            if not ok(t):
                return
            q, j = divmod(t, 2)
            if j == 0:
                g_sb[q] = rot3.tile([P, 2 * F], F32, name="g_sb", tag="g_sb")
            if t == NT - 1:
                product(nc.gpsimd, t, 0, F // 4)
                product(nc.vector, t, F // 4, F)
            else:
                product(nc.gpsimd, t, 0, F)
            if j == 1:
                store_g(q)

        def g_cast_a(q):
            if not 0 <= q < NQ - 1:
                return
            gb_sb[q] = rot2.tile([P, 2 * F], BF16, name="gb_sb", tag="gb_sb")
            vcopy(out=gb_sb[q][:, 0:384], in_=g_sb[q][:, 0:384])

        def g_cast_b(q):
            if not 0 <= q < NQ - 1:
                return
            if q == NQ - 2:
                scopy(out=gb_sb[q][:, 384 : 2 * F], in_=g_sb[q][:, 384 : 2 * F])
                return
            nc.gpsimd.tensor_scalar(
                out=gb_sb[q][:, 384 : 2 * F],
                in0=g_sb[q][:, 384 : 2 * F],
                scalar1=1.0,
                scalar2=0.0,
                op0=ALU.mult,
                op1=ALU.add,
            )

        def g_transposes(q):
            if not 0 <= q < NQ - 1:
                return
            gbank[q] = ps1.tile([P, 2, 2, P], F32, name="gbank", tag="gt")
            word_transposes(gb_sb[q][:].bitcast(F32), gbank[q])

        def g_copy(q, copy):
            if not 0 <= q < NQ - 1:
                return
            word_copy(copy, z_half(q + 3, 0).bitcast(F32), gbank[q])

        def ga2_pass(out, codes, scales):
            nc.tensor.matmul_mx(
                out=out,
                lhsT=codes.bitcast(FP8X4),
                lhsT_scale=scales,
                rhs=ac[:].bitcast(FP8X4),
                rhs_scale=asc[:],
                start=True,
                stop=True,
            )

        def ga2(q):
            if not 0 <= q < NQ - 1:
                return
            if q < NQ - 4:
                obank[q] = ps1.tile([P, 4, R], F32, name="obank", tag="xo")
            else:
                obank[q] = psl.tile([P, 4, R], F32, name="obank", tag="l")
            for j in range(2):
                cols = slice(P * j, P * (j + 1))
                ga2_pass(obank[q][:, j, :], gc[q][:, cols], gs[q][:, cols])

        def o_out(q, copy):
            if not 0 <= q < NQ - 1:
                return
            o_sb = rot4.tile([P, 2 * R], F32, name="o_sb", tag="o_sb")
            copy(out=o_sb[:], in_=obank[q][:, 0:2, :].rearrange("p j r -> p (j r)"))
            nc.sync.dma_start(out=ov[:, 2 * R * q : 2 * R * (q + 1)], in_=o_sb[:])

        def last_transposes(t):
            q, j = divmod(t, 2)
            gbank[t] = psm.tile([P, 4, P], F32, name="lbank", tag="mx")
            for c in range(4):
                u, e = divmod(c, 2)
                c0 = F * j + 256 * u + e
                nc.tensor.transpose(
                    gbank[t][:, c, :], g_sb[q][:, c0 : F * j + 256 * (u + 1) : 2], ident_f[:]
                )

        def last_copy(t, copy):
            gg[t] = keep.tile([P, 4 * P], BF16, name="lgg%d" % t, align_bytes=64)
            copy(
                out=gg[t][:].rearrange("p (r c) -> p r c", c=4),
                in_=gbank[t][:].rearrange("p c r -> p r c"),
            )

        def last_quant(t):
            gc[t] = keep.tile([P, P], U32, name="lgc%d" % t, align_bytes=64)
            gs[t] = keep.tile([P, P], U8, name="lgs%d" % t, align_bytes=64)
            nc.vector.quantize_mx(out=gc[t][:].bitcast(FP8X4), scales=gs[t][:], in_=gg[t][:])

        def last_out(t, copy):
            ob = psm.tile([P, 4, R], F32, name="lob", tag="mx")
            ga2_pass(ob[:, 0, :], gc[t][:], gs[t][:])
            o_sb = keep.tile([P, R], F32, name="lo_sb%d" % t)
            copy(out=o_sb[:], in_=ob[:, 0, :])
            nc.sync.dma_start(out=ov[:, R * t : R * (t + 1)], in_=o_sb[:])

        warm = keep.tile([P, F], BF16, name="warm")
        nc.vector.memset(warm[:], 0.0)
        wps = ps1.tile([P, F], F32, name="wps", tag="xo")

        def keep_warm(n=1):
            for i in range(n):
                nc.tensor.matmul(out=wps[:], lhsT=warm[:, 0:P], rhs=warm[:], start=True, stop=True)

        keep_warm(WARM)

        dummy = keep.tile([P, 1], F32, name="dummy")
        nc.scalar.activation(out=dummy[:], in_=ident_f[:, 0:1], func=ACT.Silu)

        w_transposes(1, psm, "mx", 0)
        w_transposes(1, psm, "mx", 1)
        keep_warm()
        w_copy(1, 0, scopy)
        w_copy(1, 1, vcopy)
        x_transposes(0)
        x_copy(0, scopy)
        w_quant(1)
        w_transposes(3, psl, "l", 0)
        keep_warm()
        w_transposes(3, psl, "l", 1)
        keep_warm()
        w_copy(3, 0, scopy)
        z_quant(-2)
        w_copy(3, 1, vcopy)
        b_transposes()
        mx_pass(1, 0)
        xa_transposes(0)
        b_copy(0, scopy)
        w_quant(3)
        xa_copy(0, vcopy)
        b_copy(1, scopy)
        mx_out(1, 0)
        mx_pass(1, 1)
        x_transposes(1)
        x_copy(1, scopy)
        lora(1, 0)
        mx_out(1, 1)
        x_transposes(2, "gt")
        x_copy(2, scopy)
        xa_transposes(1)
        add(1, 0)
        z_quant(-1)
        xa_copy(1, vcopy)
        mx_pass(3, 0)
        lora(1, 1)
        lora(3, 0)
        add(1, 1)
        mx_out(3, 0)
        silu(0)
        mx_pass(1, 2)
        lora(1, 2)
        x_transposes(3)
        mx_pass(3, 1)
        xa_transposes(2)

        for q in range(NQ):
            a, b, a2, b2, a4 = 2 * q, 2 * q + 1, 2 * q + 2, 2 * q + 3, 2 * q + 4
            z_quant(q)
            g_cast_a(q - 1)
            if q == 2:
                a2_quant()
            mx_out(1, a2)
            if q > 0:
                xa_transposes(q + 2)
            g_transposes(q - 2)
            if q == 1:
                a2_transposes()
            gate(a - 1)
            add(3, a)
            gate(a)
            mx_pass(3, a2)
            if q > 0:
                lora(1, a2)
            mx_out(3, b)
            if q < NQ - 1:
                g_cast_b(q - 1)
            mx_pass(1, b2)
            lora(3, b)
            if q > 0:
                add(1, b)
            x_copy(q + 3, vcopy if q == 0 else scopy)
            xa_copy(q + 2, vcopy)
            g_copy(q - 2, vcopy)
            if q == 1:
                a2_copy()
            mx_out(3, a2)
            silu(b)
            add(1, a2)
            x_transposes(q + 4)
            ga2(q - 3)
            mx_pass(1, a4)
            lora(3, a2)
            mx_out(1, b2)
            if q < NQ - 1:
                o_out(q - 3, vcopy if q % 3 == 0 else scopy)
            silu(a2)
            add(3, b)
            mx_pass(3, b2)
            lora(1, b2)

        t = NT - 1
        wps_end = ps1.tile([P, F], F32, name="wps_end", tag="xo")
        for i in range(3):
            nc.tensor.matmul(out=wps_end[:], lhsT=warm[:, 0:P], rhs=warm[:], start=True, stop=True)
        last_transposes(t - 1)
        g_cast_b(NQ - 2)
        z_quant(NQ)
        gate(t)
        g_transposes(NQ - 2)
        last_transposes(t)
        ga2(NQ - 3)
        o_out(NQ - 4, vcopy)
        last_copy(t - 1, scopy)
        g_copy(NQ - 2, vcopy)
        last_copy(t, scopy)
        o_out(NQ - 3, scopy)
        last_quant(t - 1)
        z_quant(NQ + 1)
        last_quant(t)
        last_out(t - 1, scopy)
        ga2(NQ - 2)
        o_out(NQ - 2, vcopy)
        last_out(t, scopy)
